import numpy as np
import ml_dtypes


def mxq(x, axis, fmt="e4m3"):
    dtype, down = {"e4m3": (ml_dtypes.float8_e4m3fn, 7), "e5m2": (ml_dtypes.float8_e5m2, 14)}[fmt]
    v = np.moveaxis(np.asarray(x, np.float32).astype(ml_dtypes.bfloat16).astype(np.float64), axis, -1)
    blocks = v.reshape(v.shape[:-1] + (-1, 32))
    amax = np.abs(blocks).max(-1, keepdims=True)
    byte = np.maximum(np.where(amax > 0, np.frexp(amax)[1] - 1 + 127, 0) - down, 1)
    scale = np.exp2(byte - 127.0)
    codes = (blocks / scale).astype(np.float32).astype(dtype).astype(np.float64)
    return np.moveaxis((codes * scale).reshape(v.shape), -1, axis)


WIDE = False


def mx_kscale(k):
    if not WIDE:
        return np.ones(k)
    levels = np.array([10, -10, 5, -5, 0])
    a = np.random.permutation(np.resize(levels, k // 512 * 4)).reshape(k // 512, 4)
    idx = np.arange(k)
    return np.exp2(a[idx // 512, idx % 128 // 32])


BF16 = ml_dtypes.bfloat16


def bf(x):
    return np.asarray(x, np.float32).astype(BF16)


def f64(x):
    return np.asarray(x).astype(np.float64)


B, DIN, NU, N, ORDER = 4, 128, 256, 512, 3
C = DIN + NU
KC = (ORDER + 1) * C


def sigmoid(v):
    return 1.0 / (1.0 + np.exp(-v))


def setup_inputs():
    sb = np.array(mx_kscale(KC)).reshape(ORDER + 1, C)
    sb[0, DIN:] = 1.0
    sb[ORDER] = sb[ORDER - 1]
    s = sb.reshape(KC)
    return {"x": bf(np.random.standard_normal((B, DIN, N)) * sb[0, :DIN, None]),
            "h_dn": bf(np.random.standard_normal((B, NU, N)) * 0.6),
            "xg1": bf(np.random.standard_normal((B, C, N)) * 0.75 * sb[1][:, None]),
            "xg2": bf(np.random.standard_normal((B, C, N)) * 0.75 * sb[ORDER - 1][:, None]),
            "adj": bf(np.random.standard_normal((N, N)) / np.sqrt(N)),
            "W_u": bf(np.random.standard_normal((NU, KC)) / np.sqrt(KC) / s),
            "b_u": bf(np.random.standard_normal(NU) * 0.2),
            "W_c": bf(np.random.standard_normal((NU, KC)) / np.sqrt(KC) / s),
            "b_c": bf(np.random.standard_normal(NU) * 0.2)}


def reference(x, h_dn, xg1, xg2, adj, W_u, b_u, W_c, b_c):
    hd = f64(h_dn)
    x2 = f64(xg2)
    xg3 = mxq(x2, 2, "e4m3") @ mxq(f64(adj), 1, "e4m3").T
    z = np.concatenate([f64(x), hd, f64(xg1), x2, xg3], axis=1)
    zq = mxq(z, 1, "e4m3")
    u = sigmoid((mxq(f64(W_u), 1, "e4m3") @ zq) + f64(b_u)[None, :, None])
    c = np.tanh((mxq(f64(W_c), 1, "e4m3") @ zq) + f64(b_c)[None, :, None])
    return u * hd + (1.0 - u) * c

@@ -1,0 +1,250 @@
+from contextlib import ExitStack
+
+import concourse.mybir as mybir
+from concourse.masks import make_identity
+
+F32 = mybir.dt.float32
+BF16 = mybir.dt.bfloat16
+U32 = mybir.dt.uint32
+U8 = mybir.dt.uint8
+FP8X4 = mybir.dt.float8_e4m3fn_x4
+ACT = mybir.ActivationFunctionType
+ALU = mybir.AluOpType
+
+P = 128
+PACK = 4
+K_PASS = P * PACK
+BATCH = 4
+NODES = 512
+NODE_CHUNKS = NODES // P
+WIDE_CH = 384
+WIDE_PARTS = WIDE_CH // PACK
+OUT_TILES = 2
+GATE_TILES = 2 * OUT_TILES
+PASSES = 3
+
+FLOPS = 2 * BATCH * WIDE_CH * NODES * NODES + 2 * 2 * BATCH * OUT_TILES * P * PASSES * K_PASS * NODES
+
+
+def tile_gcgrucell_epsilon_pb_kernel(tc, x, h_dn, xg1, xg2, adj, W_u, b_u, W_c, b_c, out):
+    nc = tc.nc
+    with ExitStack() as ctx:
+        const = ctx.enter_context(tc.tile_pool(name="const", bufs=1))
+        inputs = ctx.enter_context(tc.tile_pool(name="inputs", bufs=1))
+        work = ctx.enter_context(tc.tile_pool(name="work", bufs=2))
+        turn_psum = ctx.enter_context(tc.psum_pool(name="turn_psum", bufs=2))
+        hop_psum = ctx.enter_context(tc.psum_pool(name="hop_psum", bufs=2))
+        gate_psum = ctx.enter_context(tc.psum_pool(name="gate_psum", bufs=GATE_TILES))
+
+        ident_f32 = const.tile([P, P], F32)
+        make_identity(nc, ident_f32[:])
+        ident_bf16 = const.tile([P, P], BF16)
+        make_identity(nc, ident_bf16[:])
+
+        def four_rows_a_partition(rows):
+            return rows.rearrange("(p j) n -> p j n", j=PACK)
+
+        def load_pass(name, b, wide, narrow):
+            raw = inputs.tile([P, PACK, NODES], BF16, name="%s_%d" % (name, b))
+            if wide is not None:
+                nc.sync.dma_start(out=raw[0:WIDE_PARTS], in_=four_rows_a_partition(wide))
+            nc.sync.dma_start(out=raw[WIDE_PARTS:P], in_=four_rows_a_partition(narrow))
+            return raw
+
+        adj_raw = const.tile([P, NODE_CHUNKS, NODES], BF16)
+        nc.sync.dma_start(out=adj_raw[:], in_=adj.rearrange("(c w) v -> w c v", w=P))
+
+        raw_xg1, raw_xg2, raw_xg3, h_rows = {}, {}, {}, {}
+        raw_xg2[0] = load_pass("raw_xg2", 0, xg2[0], h_dn[0, 0:P])
+
+        w_raw = const.tile([P, GATE_TILES, PASSES, K_PASS], BF16)
+        for g in range(GATE_TILES):
+            weight = (W_u, W_c)[g // OUT_TILES]
+            rows = weight[(g % OUT_TILES) * P : (g % OUT_TILES + 1) * P, :]
+            nc.sync.dma_start(
+                out=w_raw[:, g, :, 0:WIDE_CH],
+                in_=rows[:, PASSES * P :].rearrange("o (s c) -> o s c", s=PASSES),
+            )
+            nc.sync.dma_start(
+                out=w_raw[:, g, :, WIDE_CH:K_PASS],
+                in_=rows[:, 0 : PASSES * P].rearrange("o (s c) -> o s c", s=PASSES),
+            )
+
+        bias_rows = const.tile([P, P], BF16)
+        nc.vector.memset(bias_rows[:], 0.0)
+        nc.sync.dma_start(out=bias_rows[0:OUT_TILES, :], in_=b_u.rearrange("(r o) -> r o", o=P))
+        nc.sync.dma_start(out=bias_rows[OUT_TILES:GATE_TILES, :], in_=b_c.rearrange("(r o) -> r o", o=P))
+
+        for b in range(BATCH):
+            raw_xg1[b] = load_pass("raw_xg1", b, xg1[b], x[b])
+            raw_xg3[b] = load_pass("raw_xg3", b, None, h_dn[b, P : 2 * P])
+            if b + 1 < BATCH:
+                raw_xg2[b + 1] = load_pass("raw_xg2", b + 1, xg2[b + 1], h_dn[b + 1, 0:P])
+            h_rows[b] = inputs.tile([P, OUT_TILES, NODES], BF16, name="h_rows_%d" % b)
+            nc.sync.dma_start(out=h_rows[b][:], in_=h_dn[b].rearrange("(t o) n -> o t n", o=P))
+
+        def k_onto_partitions(sources, grouped, copy):
+            turned = turn_psum.tile([P, 2, 2, P], F32, tag="turned")
+            for a in range(2):
+                words = sources[a].bitcast(F32).rearrange("r (p u) -> r u p", u=2)
+                for u in range(2):
+                    nc.tensor.transpose(turned[:, a, u, :], words[:, u, :], ident_f32[:])
+            copy(out=grouped.bitcast(F32), in_=turned[:].rearrange("p a u r -> p a r u"))
+
+        adj_grouped = const.tile([P, NODE_CHUNKS, P, PACK], BF16, align_bytes=64)
+        adj_codes = const.tile([P, NODES], U32, align_bytes=64)
+        adj_scales = const.tile([P, NODES], U8, align_bytes=64)
+        for c in range(0, NODE_CHUNKS, 2):
+            k_onto_partitions(
+                [adj_raw[:, c, :], adj_raw[:, c + 1, :]], adj_grouped[:, c : c + 2], nc.vector.tensor_copy
+            )
+        nc.vector.quantize_mx(
+            out=adj_codes[:].bitcast(FP8X4),
+            scales=adj_scales[:],
+            in_=adj_grouped[:].rearrange("p c w t -> p (c w t)"),
+        )
+
+        def quantise_xg2_for_hop(b):
+            grouped = work.tile([P, PACK, P, PACK], BF16, name="hop_grouped", align_bytes=64)
+            codes = work.tile([P, PACK, P], U32, name="hop_codes", align_bytes=64)
+            scales = work.tile([P, PACK, P], U8, name="hop_scales", align_bytes=64)
+            for j in range(0, PACK, 2):
+                k_onto_partitions(
+                    [raw_xg2[b][:, j, :], raw_xg2[b][:, j + 1, :]], grouped[:, j : j + 2], nc.scalar.copy
+                )
+            nc.vector.quantize_mx(
+                out=codes[:].rearrange("p j m -> p (j m)").bitcast(FP8X4),
+                scales=scales[:].rearrange("p j m -> p (j m)"),
+                in_=grouped[:].rearrange("p j m t -> p (j m t)"),
+            )
+            return codes, scales
+
+        w_grouped = const.tile([P, PASSES, GATE_TILES, P, PACK], BF16, align_bytes=64)
+        w_codes = const.tile([P, PASSES, GATE_TILES, P], U32, align_bytes=64)
+        w_scales = const.tile([P, PASSES, GATE_TILES, P], U8, align_bytes=64)
+
+        def quantise_weights():
+            for s in range(PASSES):
+                for g in range(0, GATE_TILES, 2):
+                    k_onto_partitions(
+                        [w_raw[:, g, s, :], w_raw[:, g + 1, s, :]], w_grouped[:, s, g : g + 2], nc.scalar.copy
+                    )
+                nc.vector.quantize_mx(
+                    out=w_codes[:, s].rearrange("p g o -> p (g o)").bitcast(FP8X4),
+                    scales=w_scales[:, s].rearrange("p g o -> p (g o)"),
+                    in_=w_grouped[:, s].rearrange("p g o t -> p (g o t)"),
+                )
+
+        bias = const.tile([P, GATE_TILES], F32)
+
+        def spread_bias():
+            bias_turned = turn_psum.tile([P, P], BF16, tag="turned")
+            nc.tensor.transpose(bias_turned[:], bias_rows[:], ident_bf16[:])
+            nc.vector.tensor_copy(out=bias[:], in_=bias_turned[:, 0:GATE_TILES])
+
+        def side_by_side(copy, grouped, raw):
+            copy(
+                out=grouped.rearrange("p (c i) j -> p c j i", i=4),
+                in_=raw.rearrange("p j (c i) -> p c j i", i=4),
+            )
+
+        def quantise_loaded_passes(b):
+            grouped = work.tile([P, 2, NODES, PACK], BF16, name="z01_grouped", align_bytes=64)
+            codes = work.tile([P, 2, NODES], U32, name="z01_codes", align_bytes=64)
+            scales = work.tile([P, 2, NODES], U8, name="z01_scales", align_bytes=64)
+            side_by_side(nc.vector.tensor_copy, grouped[:, 0], raw_xg1[b][:])
+            side_by_side(nc.vector.tensor_copy, grouped[:, 1], raw_xg2[b][:])
+            nc.vector.quantize_mx(
+                out=codes[:].rearrange("p s n -> p (s n)").bitcast(FP8X4),
+                scales=scales[:].rearrange("p s n -> p (s n)"),
+                in_=grouped[:].rearrange("p s n t -> p (s n t)"),
+            )
+            hop_pass = work.tile([P, NODES, PACK], BF16, name="z2_grouped", align_bytes=64)
+            side_by_side(nc.scalar.copy, hop_pass[WIDE_PARTS:P], raw_xg3[b][WIDE_PARTS:P])
+            return codes, scales, hop_pass
+
+        def hop(hop_codes, hop_scales, hop_pass):
+            for c in range(NODE_CHUNKS):
+                cols = slice(c * P, (c + 1) * P)
+                hopped = hop_psum.tile([P, PACK, P], F32, tag="hopped")
+                for j in range(PACK):
+                    nc.tensor.matmul_mx(
+                        out=hopped[:, j, :],
+                        lhsT=hop_codes[:, j, :].bitcast(FP8X4),
+                        lhsT_scale=hop_scales[:, j, :],
+                        rhs=adj_codes[:, cols].bitcast(FP8X4),
+                        rhs_scale=adj_scales[:, cols],
+                        start=True,
+                        stop=True,
+                    )
+                nc.scalar.copy(
+                    out=hop_pass[0:WIDE_PARTS, cols, :],
+                    in_=hopped[0:WIDE_PARTS].rearrange("p j w -> p w j"),
+                )
+            codes = work.tile([P, NODES], U32, name="z2_codes", align_bytes=64)
+            scales = work.tile([P, NODES], U8, name="z2_scales", align_bytes=64)
+            nc.vector.quantize_mx(
+                out=codes[:].bitcast(FP8X4),
+                scales=scales[:],
+                in_=hop_pass[:].rearrange("p n t -> p (n t)"),
+            )
+            return codes, scales
+
+        def gates(b, z_operands):
+            sums = [gate_psum.tile([P, NODES], F32, name="sums_%d" % g, tag="sums") for g in range(GATE_TILES)]
+            for s in range(PASSES):
+                z_codes, z_scales = z_operands[s]
+                for g in range(GATE_TILES):
+                    nc.tensor.matmul_mx(
+                        out=sums[g][:],
+                        lhsT=w_codes[:, s, g, :].bitcast(FP8X4),
+                        lhsT_scale=w_scales[:, s, g, :],
+                        rhs=z_codes.bitcast(FP8X4),
+                        rhs_scale=z_scales,
+                        start=(s == 0),
+                        stop=(s == PASSES - 1),
+                    )
+            update = work.tile([P, OUT_TILES, NODES], F32, name="update")
+            candidate = work.tile([P, OUT_TILES, NODES], F32, name="candidate")
+            for t in range(OUT_TILES):
+                nc.scalar.activation(
+                    out=update[:, t, :], in_=sums[t][:], func=ACT.Sigmoid, bias=bias[:, t : t + 1], scale=1.0
+                )
+                nc.scalar.activation(
+                    out=candidate[:, t, :],
+                    in_=sums[OUT_TILES + t][:],
+                    func=ACT.Tanh,
+                    bias=bias[:, OUT_TILES + t : OUT_TILES + t + 1],
+                    scale=1.0,
+                )
+            return update, candidate
+
+        def blend(b, update, candidate):
+            mixed = work.tile([P, OUT_TILES, NODES], F32, name="mixed")
+            for t in range(OUT_TILES):
+                nc.vector.tensor_tensor(out=mixed[:, t], in0=h_rows[b][:, t], in1=candidate[:, t], op=ALU.subtract)
+            for t in range(OUT_TILES):
+                nc.vector.tensor_tensor(out=mixed[:, t], in0=mixed[:, t], in1=update[:, t], op=ALU.mult)
+            for t in range(OUT_TILES):
+                nc.vector.tensor_tensor(out=mixed[:, t], in0=mixed[:, t], in1=candidate[:, t], op=ALU.add)
+            nc.sync.dma_start(out=out[b].rearrange("(t o) n -> o t n", o=P), in_=mixed[:])
+
+        hop_operands = quantise_xg2_for_hop(0)
+        quantise_weights()
+        spread_bias()
+        loaded = quantise_loaded_passes(0)
+        for b in range(BATCH):
+            z01_codes, z01_scales, hop_pass = loaded
+            z2_codes, z2_scales = hop(hop_operands[0], hop_operands[1], hop_pass)
+            if b + 1 < BATCH:
+                hop_operands = quantise_xg2_for_hop(b + 1)
+                loaded = quantise_loaded_passes(b + 1)
+            update, candidate = gates(
+                b,
+                [
+                    (z01_codes[:, 0, :], z01_scales[:, 0, :]),
+                    (z01_codes[:, 1, :], z01_scales[:, 1, :]),
+                    (z2_codes[:], z2_scales[:]),
+                ],
+            )
+            blend(b, update, candidate)

@@ -29,6 +29,7 @@ FLOPS = 2 * BATCH * WIDE_CH * NODES * NODES + 2 * 2 * BATCH * OUT_TILES * P * PA
 def tile_gcgrucell_epsilon_pb_kernel(tc, x, h_dn, xg1, xg2, adj, W_u, b_u, W_c, b_c, out):
     nc = tc.nc
     with ExitStack() as ctx:
+        ctx.enter_context(tc.manual_schedule())
         const = ctx.enter_context(tc.tile_pool(name="const", bufs=1))
         inputs = ctx.enter_context(tc.tile_pool(name="inputs", bufs=1))
         work = ctx.enter_context(tc.tile_pool(name="work", bufs=2))
@@ -41,6 +42,10 @@ def tile_gcgrucell_epsilon_pb_kernel(tc, x, h_dn, xg1, xg2, adj, W_u, b_u, W_c, 
         ident_bf16 = const.tile([P, P], BF16)
         make_identity(nc, ident_bf16[:])
 
+        warm = const.tile([P, 1], F32)
+        nc.vector.memset(warm[:], 0.0)
+        nc.scalar.activation(out=warm[:], in_=warm[:], func=ACT.Sigmoid)
+
         def four_rows_a_partition(rows):
             return rows.rearrange("(p j) n -> p j n", j=PACK)
 
@@ -51,11 +56,20 @@ def tile_gcgrucell_epsilon_pb_kernel(tc, x, h_dn, xg1, xg2, adj, W_u, b_u, W_c, 
             nc.sync.dma_start(out=raw[WIDE_PARTS:P], in_=four_rows_a_partition(narrow))
             return raw
 
+        raw_xg1, raw_xg2, raw_xg3, h_rows = {}, {}, {}, {}
+
+        def load_batch(b):
+            raw_xg2[b] = load_pass("raw_xg2", b, xg2[b], h_dn[b, 0:P])
+            raw_xg3[b] = load_pass("raw_xg3", b, None, h_dn[b, P : 2 * P])
+            raw_xg1[b] = load_pass("raw_xg1", b, xg1[b], x[b])
+
+        def load_h_rows(b):
+            h_rows[b] = inputs.tile([P, OUT_TILES, NODES], BF16, name="h_rows_%d" % b)
+            nc.sync.dma_start(out=h_rows[b][:], in_=h_dn[b].rearrange("(t o) n -> o t n", o=P))
+
         adj_raw = const.tile([P, NODE_CHUNKS, NODES], BF16)
         nc.sync.dma_start(out=adj_raw[:], in_=adj.rearrange("(c w) v -> w c v", w=P))
-
-        raw_xg1, raw_xg2, raw_xg3, h_rows = {}, {}, {}, {}
-        raw_xg2[0] = load_pass("raw_xg2", 0, xg2[0], h_dn[0, 0:P])
+        load_batch(0)
 
         w_raw = const.tile([P, GATE_TILES, PASSES, K_PASS], BF16)
         for g in range(GATE_TILES):
@@ -75,13 +89,10 @@ def tile_gcgrucell_epsilon_pb_kernel(tc, x, h_dn, xg1, xg2, adj, W_u, b_u, W_c, 
         nc.sync.dma_start(out=bias_rows[0:OUT_TILES, :], in_=b_u.rearrange("(r o) -> r o", o=P))
         nc.sync.dma_start(out=bias_rows[OUT_TILES:GATE_TILES, :], in_=b_c.rearrange("(r o) -> r o", o=P))
 
-        for b in range(BATCH):
-            raw_xg1[b] = load_pass("raw_xg1", b, xg1[b], x[b])
-            raw_xg3[b] = load_pass("raw_xg3", b, None, h_dn[b, P : 2 * P])
-            if b + 1 < BATCH:
-                raw_xg2[b + 1] = load_pass("raw_xg2", b + 1, xg2[b + 1], h_dn[b + 1, 0:P])
-            h_rows[b] = inputs.tile([P, OUT_TILES, NODES], BF16, name="h_rows_%d" % b)
-            nc.sync.dma_start(out=h_rows[b][:], in_=h_dn[b].rearrange("(t o) n -> o t n", o=P))
+        for b in range(1, BATCH):
+            load_batch(b)
+            load_h_rows(b - 1)
+        load_h_rows(BATCH - 1)
 
         def k_onto_partitions(sources, grouped, copy):
             turned = turn_psum.tile([P, 2, 2, P], F32, tag="turned")
@@ -94,24 +105,29 @@ def tile_gcgrucell_epsilon_pb_kernel(tc, x, h_dn, xg1, xg2, adj, W_u, b_u, W_c, 
         adj_grouped = const.tile([P, NODE_CHUNKS, P, PACK], BF16, align_bytes=64)
         adj_codes = const.tile([P, NODES], U32, align_bytes=64)
         adj_scales = const.tile([P, NODES], U8, align_bytes=64)
-        for c in range(0, NODE_CHUNKS, 2):
-            k_onto_partitions(
-                [adj_raw[:, c, :], adj_raw[:, c + 1, :]], adj_grouped[:, c : c + 2], nc.vector.tensor_copy
-            )
-        nc.vector.quantize_mx(
-            out=adj_codes[:].bitcast(FP8X4),
-            scales=adj_scales[:],
-            in_=adj_grouped[:].rearrange("p c w t -> p (c w t)"),
-        )
 
-        def quantise_xg2_for_hop(b):
+        def quantise_adj():
+            for c in range(0, NODE_CHUNKS, 2):
+                k_onto_partitions(
+                    [adj_raw[:, c, :], adj_raw[:, c + 1, :]], adj_grouped[:, c : c + 2], nc.vector.tensor_copy
+                )
+            nc.vector.quantize_mx(
+                out=adj_codes[:].bitcast(FP8X4),
+                scales=adj_scales[:],
+                in_=adj_grouped[:].rearrange("p c w t -> p (c w t)"),
+            )
+
+        def turn_xg2(b):
             grouped = work.tile([P, PACK, P, PACK], BF16, name="hop_grouped", align_bytes=64)
-            codes = work.tile([P, PACK, P], U32, name="hop_codes", align_bytes=64)
-            scales = work.tile([P, PACK, P], U8, name="hop_scales", align_bytes=64)
             for j in range(0, PACK, 2):
                 k_onto_partitions(
                     [raw_xg2[b][:, j, :], raw_xg2[b][:, j + 1, :]], grouped[:, j : j + 2], nc.scalar.copy
                 )
+            return grouped
+
+        def quantise_turned_xg2(grouped):
+            codes = work.tile([P, PACK, P], U32, name="hop_codes", align_bytes=64)
+            scales = work.tile([P, PACK, P], U8, name="hop_scales", align_bytes=64)
             nc.vector.quantize_mx(
                 out=codes[:].rearrange("p j m -> p (j m)").bitcast(FP8X4),
                 scales=scales[:].rearrange("p j m -> p (j m)"),
@@ -124,16 +140,18 @@ def tile_gcgrucell_epsilon_pb_kernel(tc, x, h_dn, xg1, xg2, adj, W_u, b_u, W_c, 
         w_scales = const.tile([P, PASSES, GATE_TILES, P], U8, align_bytes=64)
 
         def quantise_weights():
-            for s in range(PASSES):
-                for g in range(0, GATE_TILES, 2):
+            for s in range(PASSES + 1):
+                if s < PASSES:
+                    k_onto_partitions([w_raw[:, 0, s, :], w_raw[:, 1, s, :]], w_grouped[:, s, 0:2], nc.scalar.copy)
                     k_onto_partitions(
-                        [w_raw[:, g, s, :], w_raw[:, g + 1, s, :]], w_grouped[:, s, g : g + 2], nc.scalar.copy
+                        [w_raw[:, 2, s, :], w_raw[:, 3, s, :]], w_grouped[:, s, 2:4], nc.vector.tensor_copy
                     )
-                nc.vector.quantize_mx(
-                    out=w_codes[:, s].rearrange("p g o -> p (g o)").bitcast(FP8X4),
-                    scales=w_scales[:, s].rearrange("p g o -> p (g o)"),
-                    in_=w_grouped[:, s].rearrange("p g o t -> p (g o t)"),
-                )
+                if s > 0:
+                    nc.vector.quantize_mx(
+                        out=w_codes[:, s - 1].rearrange("p g o -> p (g o)").bitcast(FP8X4),
+                        scales=w_scales[:, s - 1].rearrange("p g o -> p (g o)"),
+                        in_=w_grouped[:, s - 1].rearrange("p g o t -> p (g o t)"),
+                    )
 
         bias = const.tile([P, GATE_TILES], F32)
 
@@ -148,22 +166,17 @@ def tile_gcgrucell_epsilon_pb_kernel(tc, x, h_dn, xg1, xg2, adj, W_u, b_u, W_c, 
                 in_=raw.rearrange("p j (c i) -> p c j i", i=4),
             )
 
-        def quantise_loaded_passes(b):
-            grouped = work.tile([P, 2, NODES, PACK], BF16, name="z01_grouped", align_bytes=64)
+        def quantise_loaded_passes(grouped):
             codes = work.tile([P, 2, NODES], U32, name="z01_codes", align_bytes=64)
             scales = work.tile([P, 2, NODES], U8, name="z01_scales", align_bytes=64)
-            side_by_side(nc.vector.tensor_copy, grouped[:, 0], raw_xg1[b][:])
-            side_by_side(nc.vector.tensor_copy, grouped[:, 1], raw_xg2[b][:])
             nc.vector.quantize_mx(
                 out=codes[:].rearrange("p s n -> p (s n)").bitcast(FP8X4),
                 scales=scales[:].rearrange("p s n -> p (s n)"),
                 in_=grouped[:].rearrange("p s n t -> p (s n t)"),
             )
-            hop_pass = work.tile([P, NODES, PACK], BF16, name="z2_grouped", align_bytes=64)
-            side_by_side(nc.scalar.copy, hop_pass[WIDE_PARTS:P], raw_xg3[b][WIDE_PARTS:P])
-            return codes, scales, hop_pass
+            return codes, scales
 
-        def hop(hop_codes, hop_scales, hop_pass):
+        def hop(hop_codes, hop_scales, z2_grouped):
             for c in range(NODE_CHUNKS):
                 cols = slice(c * P, (c + 1) * P)
                 hopped = hop_psum.tile([P, PACK, P], F32, tag="hopped")
@@ -178,7 +191,7 @@ def tile_gcgrucell_epsilon_pb_kernel(tc, x, h_dn, xg1, xg2, adj, W_u, b_u, W_c, 
                         stop=True,
                     )
                 nc.scalar.copy(
-                    out=hop_pass[0:WIDE_PARTS, cols, :],
+                    out=z2_grouped[0:WIDE_PARTS, cols, :],
                     in_=hopped[0:WIDE_PARTS].rearrange("p j w -> p w j"),
                 )
             codes = work.tile([P, NODES], U32, name="z2_codes", align_bytes=64)
@@ -186,17 +199,20 @@ def tile_gcgrucell_epsilon_pb_kernel(tc, x, h_dn, xg1, xg2, adj, W_u, b_u, W_c, 
             nc.vector.quantize_mx(
                 out=codes[:].bitcast(FP8X4),
                 scales=scales[:],
-                in_=hop_pass[:].rearrange("p n t -> p (n t)"),
+                in_=z2_grouped[:].rearrange("p n t -> p (n t)"),
             )
             return codes, scales
 
-        def gates(b, z_operands):
-            sums = [gate_psum.tile([P, NODES], F32, name="sums_%d" % g, tag="sums") for g in range(GATE_TILES)]
-            for s in range(PASSES):
-                z_codes, z_scales = z_operands[s]
-                for g in range(GATE_TILES):
+        GATE_ORDER = (2, 3, 0, 1)
+
+        def gates(z_operands):
+            gate = work.tile([P, GATE_TILES, NODES], F32, name="gate")
+            for g in GATE_ORDER:
+                sums = gate_psum.tile([P, NODES], F32, tag="sums")
+                for s in range(PASSES):
+                    z_codes, z_scales = z_operands[s]
                     nc.tensor.matmul_mx(
-                        out=sums[g][:],
+                        out=sums[:],
                         lhsT=w_codes[:, s, g, :].bitcast(FP8X4),
                         lhsT_scale=w_scales[:, s, g, :],
                         rhs=z_codes.bitcast(FP8X4),
@@ -204,22 +220,17 @@ def tile_gcgrucell_epsilon_pb_kernel(tc, x, h_dn, xg1, xg2, adj, W_u, b_u, W_c, 
                         start=(s == 0),
                         stop=(s == PASSES - 1),
                     )
-            update = work.tile([P, OUT_TILES, NODES], F32, name="update")
-            candidate = work.tile([P, OUT_TILES, NODES], F32, name="candidate")
-            for t in range(OUT_TILES):
                 nc.scalar.activation(
-                    out=update[:, t, :], in_=sums[t][:], func=ACT.Sigmoid, bias=bias[:, t : t + 1], scale=1.0
-                )
-                nc.scalar.activation(
-                    out=candidate[:, t, :],
-                    in_=sums[OUT_TILES + t][:],
-                    func=ACT.Tanh,
-                    bias=bias[:, OUT_TILES + t : OUT_TILES + t + 1],
+                    out=gate[:, g, :],
+                    in_=sums[:],
+                    func=(ACT.Sigmoid if g < OUT_TILES else ACT.Tanh),
+                    bias=bias[:, g : g + 1],
                     scale=1.0,
                 )
-            return update, candidate
+            return gate
 
-        def blend(b, update, candidate):
+        def blend(b, gate):
+            update, candidate = gate[:, 0:OUT_TILES], gate[:, OUT_TILES:GATE_TILES]
             mixed = work.tile([P, OUT_TILES, NODES], F32, name="mixed")
             for t in range(OUT_TILES):
                 nc.vector.tensor_tensor(out=mixed[:, t], in0=h_rows[b][:, t], in1=candidate[:, t], op=ALU.subtract)
@@ -227,24 +238,33 @@ def tile_gcgrucell_epsilon_pb_kernel(tc, x, h_dn, xg1, xg2, adj, W_u, b_u, W_c, 
                 nc.vector.tensor_tensor(out=mixed[:, t], in0=mixed[:, t], in1=update[:, t], op=ALU.mult)
             for t in range(OUT_TILES):
                 nc.vector.tensor_tensor(out=mixed[:, t], in0=mixed[:, t], in1=candidate[:, t], op=ALU.add)
-            nc.sync.dma_start(out=out[b].rearrange("(t o) n -> o t n", o=P), in_=mixed[:])
+                nc.sync.dma_start(out=out[b, t * P : (t + 1) * P, :], in_=mixed[:, t])
 
-        hop_operands = quantise_xg2_for_hop(0)
+        def prepare(b):
+            hop_grouped = turn_xg2(b)
+            z2_grouped = work.tile([P, NODES, PACK], BF16, name="z2_grouped", align_bytes=64)
+            side_by_side(nc.scalar.copy, z2_grouped[WIDE_PARTS:P], raw_xg3[b][WIDE_PARTS:P])
+            z01_grouped = work.tile([P, 2, NODES, PACK], BF16, name="z01_grouped", align_bytes=64)
+            side_by_side(nc.vector.tensor_copy, z01_grouped[:, 1], raw_xg2[b][:])
+            side_by_side(nc.vector.tensor_copy, z01_grouped[:, 0], raw_xg1[b][:])
+            hop_codes, hop_scales = quantise_turned_xg2(hop_grouped)
+            z01_codes, z01_scales = quantise_loaded_passes(z01_grouped)
+            return hop_codes, hop_scales, z2_grouped, z01_codes, z01_scales
+
+        quantise_adj()
+        hop_codes, hop_scales, z2_grouped, z01_codes, z01_scales = prepare(0)
+        z2_codes, z2_scales = hop(hop_codes, hop_scales, z2_grouped)
         quantise_weights()
         spread_bias()
-        loaded = quantise_loaded_passes(0)
         for b in range(BATCH):
-            z01_codes, z01_scales, hop_pass = loaded
-            z2_codes, z2_scales = hop(hop_operands[0], hop_operands[1], hop_pass)
+            z_operands = [
+                (z01_codes[:, 0, :], z01_scales[:, 0, :]),
+                (z01_codes[:, 1, :], z01_scales[:, 1, :]),
+                (z2_codes[:], z2_scales[:]),
+            ]
             if b + 1 < BATCH:
-                hop_operands = quantise_xg2_for_hop(b + 1)
-                loaded = quantise_loaded_passes(b + 1)
-            update, candidate = gates(
-                b,
-                [
-                    (z01_codes[:, 0, :], z01_scales[:, 0, :]),
-                    (z01_codes[:, 1, :], z01_scales[:, 1, :]),
-                    (z2_codes[:], z2_scales[:]),
-                ],
-            )
-            blend(b, update, candidate)
+                hop_codes, hop_scales, z2_grouped, z01_codes, z01_scales = prepare(b + 1)
+            gate = gates(z_operands)
+            blend(b, gate)
+            if b + 1 < BATCH:
+                z2_codes, z2_scales = hop(hop_codes, hop_scales, z2_grouped)

@@ -22,6 +22,8 @@ WIDE_PARTS = WIDE_CH // PACK
 OUT_TILES = 2
 GATE_TILES = 2 * OUT_TILES
 PASSES = 3
+PSUM_BANKS = 8
+GATE_ORDER = (2, 3, 0, 1)
 
 FLOPS = 2 * BATCH * WIDE_CH * NODES * NODES + 2 * 2 * BATCH * OUT_TILES * P * PASSES * K_PASS * NODES
 
@@ -33,9 +35,7 @@ def tile_gcgrucell_epsilon_pb_kernel(tc, x, h_dn, xg1, xg2, adj, W_u, b_u, W_c, 
         const = ctx.enter_context(tc.tile_pool(name="const", bufs=1))
         inputs = ctx.enter_context(tc.tile_pool(name="inputs", bufs=1))
         work = ctx.enter_context(tc.tile_pool(name="work", bufs=2))
-        turn_psum = ctx.enter_context(tc.psum_pool(name="turn_psum", bufs=2))
-        hop_psum = ctx.enter_context(tc.psum_pool(name="hop_psum", bufs=2))
-        gate_psum = ctx.enter_context(tc.psum_pool(name="gate_psum", bufs=GATE_TILES))
+        psum = ctx.enter_context(tc.psum_pool(name="psum", bufs=PSUM_BANKS))
 
         ident_f32 = const.tile([P, P], F32)
         make_identity(nc, ident_f32[:])
@@ -95,7 +95,7 @@ def tile_gcgrucell_epsilon_pb_kernel(tc, x, h_dn, xg1, xg2, adj, W_u, b_u, W_c, 
         load_h_rows(BATCH - 1)
 
         def k_onto_partitions(sources, grouped, copy):
-            turned = turn_psum.tile([P, 2, 2, P], F32, tag="turned")
+            turned = psum.tile([P, 2, 2, P], F32, tag="bank")
             for a in range(2):
                 words = sources[a].bitcast(F32).rearrange("r (p u) -> r u p", u=2)
                 for u in range(2):
@@ -156,7 +156,7 @@ def tile_gcgrucell_epsilon_pb_kernel(tc, x, h_dn, xg1, xg2, adj, W_u, b_u, W_c, 
         bias = const.tile([P, GATE_TILES], F32)
 
         def spread_bias():
-            bias_turned = turn_psum.tile([P, P], BF16, tag="turned")
+            bias_turned = psum.tile([P, P], BF16, tag="bank")
             nc.tensor.transpose(bias_turned[:], bias_rows[:], ident_bf16[:])
             nc.vector.tensor_copy(out=bias[:], in_=bias_turned[:, 0:GATE_TILES])
 
@@ -176,10 +176,11 @@ def tile_gcgrucell_epsilon_pb_kernel(tc, x, h_dn, xg1, xg2, adj, W_u, b_u, W_c, 
             )
             return codes, scales
 
-        def hop(hop_codes, hop_scales, z2_grouped):
+        def hop_products(hop_codes, hop_scales):
+            banks = []
             for c in range(NODE_CHUNKS):
                 cols = slice(c * P, (c + 1) * P)
-                hopped = hop_psum.tile([P, PACK, P], F32, tag="hopped")
+                hopped = psum.tile([P, PACK, P], F32, name="hopped_%d" % c, tag="bank")
                 for j in range(PACK):
                     nc.tensor.matmul_mx(
                         out=hopped[:, j, :],
@@ -190,10 +191,17 @@ def tile_gcgrucell_epsilon_pb_kernel(tc, x, h_dn, xg1, xg2, adj, W_u, b_u, W_c, 
                         start=True,
                         stop=True,
                     )
+                banks.append(hopped)
+            return banks
+
+        def round_hop(banks, z2_grouped):
+            for c in range(NODE_CHUNKS):
                 nc.scalar.copy(
-                    out=z2_grouped[0:WIDE_PARTS, cols, :],
-                    in_=hopped[0:WIDE_PARTS].rearrange("p j w -> p w j"),
+                    out=z2_grouped[0:WIDE_PARTS, c * P : (c + 1) * P, :],
+                    in_=banks[c][0:WIDE_PARTS].rearrange("p j w -> p w j"),
                 )
+
+        def quantise_hop_pass(z2_grouped):
             codes = work.tile([P, NODES], U32, name="z2_codes", align_bytes=64)
             scales = work.tile([P, NODES], U8, name="z2_scales", align_bytes=64)
             nc.vector.quantize_mx(
@@ -203,26 +211,24 @@ def tile_gcgrucell_epsilon_pb_kernel(tc, x, h_dn, xg1, xg2, adj, W_u, b_u, W_c, 
             )
             return codes, scales
 
-        GATE_ORDER = (2, 3, 0, 1)
+        def gate_pass(sums, s, z_codes, z_scales):
+            for g in GATE_ORDER:
+                nc.tensor.matmul_mx(
+                    out=sums[g][:],
+                    lhsT=w_codes[:, s, g, :].bitcast(FP8X4),
+                    lhsT_scale=w_scales[:, s, g, :],
+                    rhs=z_codes.bitcast(FP8X4),
+                    rhs_scale=z_scales,
+                    start=(s == 0),
+                    stop=(s == PASSES - 1),
+                )
 
-        def gates(z_operands):
+        def gate_functions(sums):
             gate = work.tile([P, GATE_TILES, NODES], F32, name="gate")
             for g in GATE_ORDER:
-                sums = gate_psum.tile([P, NODES], F32, tag="sums")
-                for s in range(PASSES):
-                    z_codes, z_scales = z_operands[s]
-                    nc.tensor.matmul_mx(
-                        out=sums[:],
-                        lhsT=w_codes[:, s, g, :].bitcast(FP8X4),
-                        lhsT_scale=w_scales[:, s, g, :],
-                        rhs=z_codes.bitcast(FP8X4),
-                        rhs_scale=z_scales,
-                        start=(s == 0),
-                        stop=(s == PASSES - 1),
-                    )
                 nc.scalar.activation(
                     out=gate[:, g, :],
-                    in_=sums[:],
+                    in_=sums[g][:],
                     func=(ACT.Sigmoid if g < OUT_TILES else ACT.Tanh),
                     bias=bias[:, g : g + 1],
                     scale=1.0,
@@ -240,31 +246,41 @@ def tile_gcgrucell_epsilon_pb_kernel(tc, x, h_dn, xg1, xg2, adj, W_u, b_u, W_c, 
                 nc.vector.tensor_tensor(out=mixed[:, t], in0=mixed[:, t], in1=candidate[:, t], op=ALU.add)
                 nc.sync.dma_start(out=out[b, t * P : (t + 1) * P, :], in_=mixed[:, t])
 
-        def prepare(b):
+        def start_batch(b):
             hop_grouped = turn_xg2(b)
             z2_grouped = work.tile([P, NODES, PACK], BF16, name="z2_grouped", align_bytes=64)
             side_by_side(nc.scalar.copy, z2_grouped[WIDE_PARTS:P], raw_xg3[b][WIDE_PARTS:P])
             z01_grouped = work.tile([P, 2, NODES, PACK], BF16, name="z01_grouped", align_bytes=64)
             side_by_side(nc.vector.tensor_copy, z01_grouped[:, 1], raw_xg2[b][:])
+            return hop_grouped, z2_grouped, z01_grouped
+
+        def finish_operands(b, hop_grouped, z01_grouped):
             side_by_side(nc.vector.tensor_copy, z01_grouped[:, 0], raw_xg1[b][:])
             hop_codes, hop_scales = quantise_turned_xg2(hop_grouped)
             z01_codes, z01_scales = quantise_loaded_passes(z01_grouped)
-            return hop_codes, hop_scales, z2_grouped, z01_codes, z01_scales
+            return hop_codes, hop_scales, z01_codes, z01_scales
 
         quantise_adj()
-        hop_codes, hop_scales, z2_grouped, z01_codes, z01_scales = prepare(0)
-        z2_codes, z2_scales = hop(hop_codes, hop_scales, z2_grouped)
+        hop_grouped, z2_grouped, z01_grouped = start_batch(0)
+        hop_codes, hop_scales, z01_codes, z01_scales = finish_operands(0, hop_grouped, z01_grouped)
+        round_hop(hop_products(hop_codes, hop_scales), z2_grouped)
         quantise_weights()
         spread_bias()
         for b in range(BATCH):
-            z_operands = [
-                (z01_codes[:, 0, :], z01_scales[:, 0, :]),
-                (z01_codes[:, 1, :], z01_scales[:, 1, :]),
-                (z2_codes[:], z2_scales[:]),
-            ]
-            if b + 1 < BATCH:
-                hop_codes, hop_scales, z2_grouped, z01_codes, z01_scales = prepare(b + 1)
-            gate = gates(z_operands)
+            more = b + 1 < BATCH
+            this_z2_grouped, this_z01_codes, this_z01_scales = z2_grouped, z01_codes, z01_scales
+            if more:
+                hop_grouped, z2_grouped, z01_grouped = start_batch(b + 1)
+            z2_codes, z2_scales = quantise_hop_pass(this_z2_grouped)
+            if more:
+                hop_codes, hop_scales, z01_codes, z01_scales = finish_operands(b + 1, hop_grouped, z01_grouped)
+            sums = [psum.tile([P, NODES], F32, name="sums_%d" % g, tag="bank") for g in range(GATE_TILES)]
+            gate_pass(sums, 0, this_z01_codes[:, 0, :], this_z01_scales[:, 0, :])
+            gate_pass(sums, 1, this_z01_codes[:, 1, :], this_z01_scales[:, 1, :])
+            gate_pass(sums, 2, z2_codes[:], z2_scales[:])
+            gate = gate_functions(sums)
+            if more:
+                banks = hop_products(hop_codes, hop_scales)
             blend(b, gate)
-            if b + 1 < BATCH:
-                z2_codes, z2_scales = hop(hop_codes, hop_scales, z2_grouped)
+            if more:
+                round_hop(banks, z2_grouped)

@@ -23,6 +23,7 @@ OUT_TILES = 2
 GATE_TILES = 2 * OUT_TILES
 PASSES = 3
 PSUM_BANKS = 8
+WEIGHTS_ROUND = 3
 GATE_ORDER = (2, 3, 0, 1)
 
 FLOPS = 2 * BATCH * WIDE_CH * NODES * NODES + 2 * 2 * BATCH * OUT_TILES * P * PASSES * K_PASS * NODES
@@ -35,6 +36,8 @@ def tile_gcgrucell_epsilon_pb_kernel(tc, x, h_dn, xg1, xg2, adj, W_u, b_u, W_c, 
         const = ctx.enter_context(tc.tile_pool(name="const", bufs=1))
         inputs = ctx.enter_context(tc.tile_pool(name="inputs", bufs=1))
         work = ctx.enter_context(tc.tile_pool(name="work", bufs=2))
+        deep = ctx.enter_context(tc.tile_pool(name="deep", bufs=3))
+        ahead = ctx.enter_context(tc.tile_pool(name="ahead", bufs=BATCH))
         psum = ctx.enter_context(tc.psum_pool(name="psum", bufs=PSUM_BANKS))
 
         ident_f32 = const.tile([P, P], F32)
@@ -60,39 +63,42 @@ def tile_gcgrucell_epsilon_pb_kernel(tc, x, h_dn, xg1, xg2, adj, W_u, b_u, W_c, 
 
         def load_batch(b):
             raw_xg2[b] = load_pass("raw_xg2", b, xg2[b], h_dn[b, 0:P])
-            raw_xg3[b] = load_pass("raw_xg3", b, None, h_dn[b, P : 2 * P])
+            if b == 0:
+                nc.sync.dma_start(out=adj_raw[:], in_=adj.rearrange("(c w) v -> w c v", w=P))
             raw_xg1[b] = load_pass("raw_xg1", b, xg1[b], x[b])
+            raw_xg3[b] = load_pass("raw_xg3", b, None, h_dn[b, P : 2 * P])
 
         def load_h_rows(b):
             h_rows[b] = inputs.tile([P, OUT_TILES, NODES], BF16, name="h_rows_%d" % b)
             nc.sync.dma_start(out=h_rows[b][:], in_=h_dn[b].rearrange("(t o) n -> o t n", o=P))
 
         adj_raw = const.tile([P, NODE_CHUNKS, NODES], BF16)
-        nc.sync.dma_start(out=adj_raw[:], in_=adj.rearrange("(c w) v -> w c v", w=P))
-        load_batch(0)
-
         w_raw = const.tile([P, GATE_TILES, PASSES, K_PASS], BF16)
-        for g in range(GATE_TILES):
-            weight = (W_u, W_c)[g // OUT_TILES]
-            rows = weight[(g % OUT_TILES) * P : (g % OUT_TILES + 1) * P, :]
-            nc.sync.dma_start(
-                out=w_raw[:, g, :, 0:WIDE_CH],
-                in_=rows[:, PASSES * P :].rearrange("o (s c) -> o s c", s=PASSES),
-            )
-            nc.sync.dma_start(
-                out=w_raw[:, g, :, WIDE_CH:K_PASS],
-                in_=rows[:, 0 : PASSES * P].rearrange("o (s c) -> o s c", s=PASSES),
-            )
-
         bias_rows = const.tile([P, P], BF16)
         nc.vector.memset(bias_rows[:], 0.0)
-        nc.sync.dma_start(out=bias_rows[0:OUT_TILES, :], in_=b_u.rearrange("(r o) -> r o", o=P))
-        nc.sync.dma_start(out=bias_rows[OUT_TILES:GATE_TILES, :], in_=b_c.rearrange("(r o) -> r o", o=P))
 
-        for b in range(1, BATCH):
+        def load_weights():
+            for g in range(GATE_TILES):
+                weight = (W_u, W_c)[g // OUT_TILES]
+                rows = weight[(g % OUT_TILES) * P : (g % OUT_TILES + 1) * P, :]
+                nc.sync.dma_start(
+                    out=w_raw[:, g, :, 0:WIDE_CH],
+                    in_=rows[:, PASSES * P :].rearrange("o (s c) -> o s c", s=PASSES),
+                )
+                nc.sync.dma_start(
+                    out=w_raw[:, g, :, WIDE_CH:K_PASS],
+                    in_=rows[:, 0 : PASSES * P].rearrange("o (s c) -> o s c", s=PASSES),
+                )
+            nc.sync.dma_start(out=bias_rows[0:OUT_TILES, :], in_=b_u.rearrange("(r o) -> r o", o=P))
+            nc.sync.dma_start(out=bias_rows[OUT_TILES:GATE_TILES, :], in_=b_c.rearrange("(r o) -> r o", o=P))
+
+        for b in range(BATCH):
+            if b == WEIGHTS_ROUND:
+                load_weights()
+                load_h_rows(0)
             load_batch(b)
-            load_h_rows(b - 1)
-        load_h_rows(BATCH - 1)
+        for b in range(1, BATCH):
+            load_h_rows(b)
 
         def k_onto_partitions(sources, grouped, copy):
             turned = psum.tile([P, 2, 2, P], F32, tag="bank")
@@ -106,11 +112,11 @@ def tile_gcgrucell_epsilon_pb_kernel(tc, x, h_dn, xg1, xg2, adj, W_u, b_u, W_c, 
         adj_codes = const.tile([P, NODES], U32, align_bytes=64)
         adj_scales = const.tile([P, NODES], U8, align_bytes=64)
 
-        def quantise_adj():
+        def turn_adj():
             for c in range(0, NODE_CHUNKS, 2):
-                k_onto_partitions(
-                    [adj_raw[:, c, :], adj_raw[:, c + 1, :]], adj_grouped[:, c : c + 2], nc.vector.tensor_copy
-                )
+                k_onto_partitions([adj_raw[:, c, :], adj_raw[:, c + 1, :]], adj_grouped[:, c : c + 2], nc.scalar.copy)
+
+        def quantise_adj():
             nc.vector.quantize_mx(
                 out=adj_codes[:].bitcast(FP8X4),
                 scales=adj_scales[:],
@@ -167,8 +173,8 @@ def tile_gcgrucell_epsilon_pb_kernel(tc, x, h_dn, xg1, xg2, adj, W_u, b_u, W_c, 
             )
 
         def quantise_loaded_passes(grouped):
-            codes = work.tile([P, 2, NODES], U32, name="z01_codes", align_bytes=64)
-            scales = work.tile([P, 2, NODES], U8, name="z01_scales", align_bytes=64)
+            codes = ahead.tile([P, 2, NODES], U32, name="z01_codes", align_bytes=64)
+            scales = ahead.tile([P, 2, NODES], U8, name="z01_scales", align_bytes=64)
             nc.vector.quantize_mx(
                 out=codes[:].rearrange("p s n -> p (s n)").bitcast(FP8X4),
                 scales=scales[:].rearrange("p s n -> p (s n)"),
@@ -202,8 +208,8 @@ def tile_gcgrucell_epsilon_pb_kernel(tc, x, h_dn, xg1, xg2, adj, W_u, b_u, W_c, 
                 )
 
         def quantise_hop_pass(z2_grouped):
-            codes = work.tile([P, NODES], U32, name="z2_codes", align_bytes=64)
-            scales = work.tile([P, NODES], U8, name="z2_scales", align_bytes=64)
+            codes = ahead.tile([P, NODES], U32, name="z2_codes", align_bytes=64)
+            scales = ahead.tile([P, NODES], U8, name="z2_scales", align_bytes=64)
             nc.vector.quantize_mx(
                 out=codes[:].bitcast(FP8X4),
                 scales=scales[:],
@@ -211,20 +217,25 @@ def tile_gcgrucell_epsilon_pb_kernel(tc, x, h_dn, xg1, xg2, adj, W_u, b_u, W_c, 
             )
             return codes, scales
 
-        def gate_pass(sums, s, z_codes, z_scales):
+        def gate_sums(z_operands):
+            sums = {}
             for g in GATE_ORDER:
-                nc.tensor.matmul_mx(
-                    out=sums[g][:],
-                    lhsT=w_codes[:, s, g, :].bitcast(FP8X4),
-                    lhsT_scale=w_scales[:, s, g, :],
-                    rhs=z_codes.bitcast(FP8X4),
-                    rhs_scale=z_scales,
-                    start=(s == 0),
-                    stop=(s == PASSES - 1),
-                )
+                sums[g] = psum.tile([P, NODES], F32, name="sums_%d" % g, tag="bank")
+                for s in range(PASSES):
+                    z_codes, z_scales = z_operands[s]
+                    nc.tensor.matmul_mx(
+                        out=sums[g][:],
+                        lhsT=w_codes[:, s, g, :].bitcast(FP8X4),
+                        lhsT_scale=w_scales[:, s, g, :],
+                        rhs=z_codes.bitcast(FP8X4),
+                        rhs_scale=z_scales,
+                        start=(s == 0),
+                        stop=(s == PASSES - 1),
+                    )
+            return sums
 
         def gate_functions(sums):
-            gate = work.tile([P, GATE_TILES, NODES], F32, name="gate")
+            gate = deep.tile([P, GATE_TILES, NODES], F32, name="gate")
             for g in GATE_ORDER:
                 nc.scalar.activation(
                     out=gate[:, g, :],
@@ -246,41 +257,43 @@ def tile_gcgrucell_epsilon_pb_kernel(tc, x, h_dn, xg1, xg2, adj, W_u, b_u, W_c, 
                 nc.vector.tensor_tensor(out=mixed[:, t], in0=mixed[:, t], in1=candidate[:, t], op=ALU.add)
                 nc.sync.dma_start(out=out[b, t * P : (t + 1) * P, :], in_=mixed[:, t])
 
-        def start_batch(b):
-            hop_grouped = turn_xg2(b)
-            z2_grouped = work.tile([P, NODES, PACK], BF16, name="z2_grouped", align_bytes=64)
-            side_by_side(nc.scalar.copy, z2_grouped[WIDE_PARTS:P], raw_xg3[b][WIDE_PARTS:P])
+        hop_operands, z2_grouped, z01, z2 = {}, {}, {}, {}
+
+        def finish_hop_on_tensor_and_scalar(b):
+            round_hop(hop_products(hop_operands[b][0], hop_operands[b][1]), z2_grouped[b])
+
+        for n in range(BATCH):
+            if n == WEIGHTS_ROUND:
+                quantise_weights()
+                spread_bias()
+            hop_grouped = turn_xg2(n)
+            if n == 0:
+                turn_adj()
+            else:
+                finish_hop_on_tensor_and_scalar(n - 1)
+            z2_grouped[n] = deep.tile([P, NODES, PACK], BF16, name="z2_grouped", align_bytes=64)
+            side_by_side(nc.scalar.copy, z2_grouped[n][WIDE_PARTS:P], raw_xg3[n][WIDE_PARTS:P])
             z01_grouped = work.tile([P, 2, NODES, PACK], BF16, name="z01_grouped", align_bytes=64)
-            side_by_side(nc.vector.tensor_copy, z01_grouped[:, 1], raw_xg2[b][:])
-            return hop_grouped, z2_grouped, z01_grouped
+            side_by_side(nc.vector.tensor_copy, z01_grouped[:, 1], raw_xg2[n][:])
+            hop_operands[n] = quantise_turned_xg2(hop_grouped)
+            side_by_side(nc.vector.tensor_copy, z01_grouped[:, 0], raw_xg1[n][:])
+            if n == 0:
+                quantise_adj()
+            z01[n] = quantise_loaded_passes(z01_grouped)
+            if n > 0:
+                z2[n - 1] = quantise_hop_pass(z2_grouped[n - 1])
 
-        def finish_operands(b, hop_grouped, z01_grouped):
-            side_by_side(nc.vector.tensor_copy, z01_grouped[:, 0], raw_xg1[b][:])
-            hop_codes, hop_scales = quantise_turned_xg2(hop_grouped)
-            z01_codes, z01_scales = quantise_loaded_passes(z01_grouped)
-            return hop_codes, hop_scales, z01_codes, z01_scales
-
-        quantise_adj()
-        hop_grouped, z2_grouped, z01_grouped = start_batch(0)
-        hop_codes, hop_scales, z01_codes, z01_scales = finish_operands(0, hop_grouped, z01_grouped)
-        round_hop(hop_products(hop_codes, hop_scales), z2_grouped)
-        quantise_weights()
-        spread_bias()
         for b in range(BATCH):
-            more = b + 1 < BATCH
-            this_z2_grouped, this_z01_codes, this_z01_scales = z2_grouped, z01_codes, z01_scales
-            if more:
-                hop_grouped, z2_grouped, z01_grouped = start_batch(b + 1)
-            z2_codes, z2_scales = quantise_hop_pass(this_z2_grouped)
-            if more:
-                hop_codes, hop_scales, z01_codes, z01_scales = finish_operands(b + 1, hop_grouped, z01_grouped)
-            sums = [psum.tile([P, NODES], F32, name="sums_%d" % g, tag="bank") for g in range(GATE_TILES)]
-            gate_pass(sums, 0, this_z01_codes[:, 0, :], this_z01_scales[:, 0, :])
-            gate_pass(sums, 1, this_z01_codes[:, 1, :], this_z01_scales[:, 1, :])
-            gate_pass(sums, 2, z2_codes[:], z2_scales[:])
+            sums = gate_sums(
+                [
+                    (z01[b][0][:, 0, :], z01[b][1][:, 0, :]),
+                    (z01[b][0][:, 1, :], z01[b][1][:, 1, :]),
+                    (z2[b][0][:], z2[b][1][:]),
+                ]
+            )
             gate = gate_functions(sums)
-            if more:
-                banks = hop_products(hop_codes, hop_scales)
+            if b == 0:
+                finish_hop_on_tensor_and_scalar(BATCH - 1)
             blend(b, gate)
-            if more:
-                round_hop(banks, z2_grouped)
+            if b == 0:
+                z2[BATCH - 1] = quantise_hop_pass(z2_grouped[BATCH - 1])

@@ -19,6 +19,7 @@ NODES = 512
 NODE_CHUNKS = NODES // P
 WIDE_CH = 384
 WIDE_PARTS = WIDE_CH // PACK
+QUADRANT = 32
 OUT_TILES = 2
 GATE_TILES = 2 * OUT_TILES
 PASSES = 3
@@ -55,7 +56,8 @@ def tile_gcgrucell_epsilon_pb_kernel(tc, x, h_dn, xg1, xg2, adj, W_u, b_u, W_c, 
         def load_pass(name, b, wide, narrow):
             raw = inputs.tile([P, PACK, NODES], BF16, name="%s_%d" % (name, b))
             if wide is not None:
-                nc.sync.dma_start(out=raw[0:WIDE_PARTS], in_=four_rows_a_partition(wide))
+                nc.sync.dma_start(out=raw[QUADRANT:WIDE_PARTS], in_=four_rows_a_partition(wide[PACK * QUADRANT :]))
+                nc.sync.dma_start(out=raw[0:QUADRANT], in_=four_rows_a_partition(wide[0 : PACK * QUADRANT]))
             nc.sync.dma_start(out=raw[WIDE_PARTS:P], in_=four_rows_a_partition(narrow))
             return raw
 

@@ -24,7 +24,8 @@ OUT_TILES = 2
 GATE_TILES = 2 * OUT_TILES
 PASSES = 3
 PSUM_BANKS = 8
-WEIGHTS_ROUND = 3
+GATE_LAG = 2
+ROUNDS = BATCH + GATE_LAG
 GATE_ORDER = (2, 3, 0, 1)
 
 FLOPS = 2 * BATCH * WIDE_CH * NODES * NODES + 2 * 2 * BATCH * OUT_TILES * P * PASSES * K_PASS * NODES
@@ -94,13 +95,12 @@ def tile_gcgrucell_epsilon_pb_kernel(tc, x, h_dn, xg1, xg2, adj, W_u, b_u, W_c, 
             nc.sync.dma_start(out=bias_rows[0:OUT_TILES, :], in_=b_u.rearrange("(r o) -> r o", o=P))
             nc.sync.dma_start(out=bias_rows[OUT_TILES:GATE_TILES, :], in_=b_c.rearrange("(r o) -> r o", o=P))
 
-        for b in range(BATCH):
-            if b == WEIGHTS_ROUND:
-                load_weights()
-                load_h_rows(0)
-            load_batch(b)
-        for b in range(1, BATCH):
-            load_h_rows(b)
+        load_weights()
+        for r in range(ROUNDS):
+            if r < BATCH:
+                load_batch(r)
+            if r >= GATE_LAG:
+                load_h_rows(r - GATE_LAG)
 
         def k_onto_partitions(sources, grouped, copy):
             turned = psum.tile([P, 2, 2, P], F32, tag="bank")
@@ -148,17 +148,21 @@ def tile_gcgrucell_epsilon_pb_kernel(tc, x, h_dn, xg1, xg2, adj, W_u, b_u, W_c, 
         w_scales = const.tile([P, PASSES, GATE_TILES, P], U8, align_bytes=64)
 
         def quantise_weights():
-            for s in range(PASSES + 1):
-                if s < PASSES:
-                    k_onto_partitions([w_raw[:, 0, s, :], w_raw[:, 1, s, :]], w_grouped[:, s, 0:2], nc.scalar.copy)
+            banks = [(g, s) for g in range(0, GATE_TILES, 2) for s in range(PASSES)]
+            for i in range(len(banks) + 1):
+                if i < len(banks):
+                    g, s = banks[i]
                     k_onto_partitions(
-                        [w_raw[:, 2, s, :], w_raw[:, 3, s, :]], w_grouped[:, s, 2:4], nc.vector.tensor_copy
+                        [w_raw[:, g, s, :], w_raw[:, g + 1, s, :]],
+                        w_grouped[:, s, g : g + 2],
+                        (nc.scalar.copy, nc.vector.tensor_copy)[i % 2],
                     )
-                if s > 0:
+                if i > 0:
+                    g, s = banks[i - 1]
                     nc.vector.quantize_mx(
-                        out=w_codes[:, s - 1].rearrange("p g o -> p (g o)").bitcast(FP8X4),
-                        scales=w_scales[:, s - 1].rearrange("p g o -> p (g o)"),
-                        in_=w_grouped[:, s - 1].rearrange("p g o t -> p (g o t)"),
+                        out=w_codes[:, s, g : g + 2].rearrange("p g o -> p (g o)").bitcast(FP8X4),
+                        scales=w_scales[:, s, g : g + 2].rearrange("p g o -> p (g o)"),
+                        in_=w_grouped[:, s, g : g + 2].rearrange("p g o t -> p (g o t)"),
                     )
 
         bias = const.tile([P, GATE_TILES], F32)
@@ -261,41 +265,35 @@ def tile_gcgrucell_epsilon_pb_kernel(tc, x, h_dn, xg1, xg2, adj, W_u, b_u, W_c, 
 
         hop_operands, z2_grouped, z01, z2 = {}, {}, {}, {}
 
-        def finish_hop_on_tensor_and_scalar(b):
-            round_hop(hop_products(hop_operands[b][0], hop_operands[b][1]), z2_grouped[b])
-
-        for n in range(BATCH):
-            if n == WEIGHTS_ROUND:
-                quantise_weights()
-                spread_bias()
-            hop_grouped = turn_xg2(n)
-            if n == 0:
-                turn_adj()
-            else:
-                finish_hop_on_tensor_and_scalar(n - 1)
-            z2_grouped[n] = deep.tile([P, NODES, PACK], BF16, name="z2_grouped", align_bytes=64)
-            side_by_side(nc.scalar.copy, z2_grouped[n][WIDE_PARTS:P], raw_xg3[n][WIDE_PARTS:P])
-            z01_grouped = work.tile([P, 2, NODES, PACK], BF16, name="z01_grouped", align_bytes=64)
-            side_by_side(nc.vector.tensor_copy, z01_grouped[:, 1], raw_xg2[n][:])
-            hop_operands[n] = quantise_turned_xg2(hop_grouped)
-            side_by_side(nc.vector.tensor_copy, z01_grouped[:, 0], raw_xg1[n][:])
-            if n == 0:
-                quantise_adj()
-            z01[n] = quantise_loaded_passes(z01_grouped)
-            if n > 0:
-                z2[n - 1] = quantise_hop_pass(z2_grouped[n - 1])
-
-        for b in range(BATCH):
-            sums = gate_sums(
-                [
-                    (z01[b][0][:, 0, :], z01[b][1][:, 0, :]),
-                    (z01[b][0][:, 1, :], z01[b][1][:, 1, :]),
-                    (z2[b][0][:], z2[b][1][:]),
-                ]
-            )
-            gate = gate_functions(sums)
-            if b == 0:
-                finish_hop_on_tensor_and_scalar(BATCH - 1)
-            blend(b, gate)
-            if b == 0:
-                z2[BATCH - 1] = quantise_hop_pass(z2_grouped[BATCH - 1])
+        quantise_weights()
+        spread_bias()
+        for r in range(ROUNDS):
+            new, hopped, done = r, r - 1, r - GATE_LAG
+            if new < BATCH:
+                hop_grouped = turn_xg2(new)
+                if new == 0:
+                    turn_adj()
+            if 0 <= hopped < BATCH:
+                round_hop(hop_products(*hop_operands[hopped]), z2_grouped[hopped])
+            if new < BATCH:
+                z2_grouped[new] = deep.tile([P, NODES, PACK], BF16, name="z2_grouped", align_bytes=64)
+                side_by_side(nc.scalar.copy, z2_grouped[new][WIDE_PARTS:P], raw_xg3[new][WIDE_PARTS:P])
+            if new < BATCH:
+                z01_grouped = work.tile([P, 2, NODES, PACK], BF16, name="z01_grouped", align_bytes=64)
+                side_by_side(nc.vector.tensor_copy, z01_grouped[:, 1], raw_xg2[new][:])
+                hop_operands[new] = quantise_turned_xg2(hop_grouped)
+                side_by_side(nc.vector.tensor_copy, z01_grouped[:, 0], raw_xg1[new][:])
+                if new == 0:
+                    quantise_adj()
+                z01[new] = quantise_loaded_passes(z01_grouped)
+            if 0 <= hopped < BATCH:
+                z2[hopped] = quantise_hop_pass(z2_grouped[hopped])
+            if done >= 0:
+                sums = gate_sums(
+                    [
+                        (z01[done][0][:, 0, :], z01[done][1][:, 0, :]),
+                        (z01[done][0][:, 1, :], z01[done][1][:, 1, :]),
+                        (z2[done][0][:], z2[done][1][:]),
+                    ]
+                )
+                blend(done, gate_functions(sums))

@@ -24,8 +24,6 @@ OUT_TILES = 2
 GATE_TILES = 2 * OUT_TILES
 PASSES = 3
 PSUM_BANKS = 8
-GATE_LAG = 2
-ROUNDS = BATCH + GATE_LAG
 GATE_ORDER = (2, 3, 0, 1)
 
 FLOPS = 2 * BATCH * WIDE_CH * NODES * NODES + 2 * 2 * BATCH * OUT_TILES * P * PASSES * K_PASS * NODES
@@ -37,9 +35,8 @@ def tile_gcgrucell_epsilon_pb_kernel(tc, x, h_dn, xg1, xg2, adj, W_u, b_u, W_c, 
         ctx.enter_context(tc.manual_schedule())
         const = ctx.enter_context(tc.tile_pool(name="const", bufs=1))
         inputs = ctx.enter_context(tc.tile_pool(name="inputs", bufs=1))
+        batches = ctx.enter_context(tc.tile_pool(name="batches", bufs=BATCH))
         work = ctx.enter_context(tc.tile_pool(name="work", bufs=2))
-        deep = ctx.enter_context(tc.tile_pool(name="deep", bufs=3))
-        ahead = ctx.enter_context(tc.tile_pool(name="ahead", bufs=BATCH))
         psum = ctx.enter_context(tc.psum_pool(name="psum", bufs=PSUM_BANKS))
 
         ident_f32 = const.tile([P, P], F32)
@@ -62,14 +59,24 @@ def tile_gcgrucell_epsilon_pb_kernel(tc, x, h_dn, xg1, xg2, adj, W_u, b_u, W_c, 
             nc.sync.dma_start(out=raw[WIDE_PARTS:P], in_=four_rows_a_partition(narrow))
             return raw
 
-        raw_xg1, raw_xg2, raw_xg3, h_rows = {}, {}, {}, {}
+        raw_xg1, raw_xg2, h_rows, z2_grouped = {}, {}, {}, {}
+        h2_raw = const.tile([P, PACK, NODES], BF16)
+        h2_grouped = const.tile([P, NODES, PACK], BF16)
 
-        def load_batch(b):
+        def load_h2():
+            for b in range(BATCH):
+                nc.sync.dma_start(
+                    out=h2_raw[b * QUADRANT : (b + 1) * QUADRANT], in_=four_rows_a_partition(h_dn[b, P : 2 * P])
+                )
+
+        def move_h2(b):
+            nc.sync.dma_start(out=z2_grouped[b][WIDE_PARTS:P], in_=h2_grouped[b * QUADRANT : (b + 1) * QUADRANT])
+
+        def load_xg2(b):
             raw_xg2[b] = load_pass("raw_xg2", b, xg2[b], h_dn[b, 0:P])
-            if b == 0:
-                nc.sync.dma_start(out=adj_raw[:], in_=adj.rearrange("(c w) v -> w c v", w=P))
+
+        def load_xg1(b):
             raw_xg1[b] = load_pass("raw_xg1", b, xg1[b], x[b])
-            raw_xg3[b] = load_pass("raw_xg3", b, None, h_dn[b, P : 2 * P])
 
         def load_h_rows(b):
             h_rows[b] = inputs.tile([P, OUT_TILES, NODES], BF16, name="h_rows_%d" % b)
@@ -92,15 +99,17 @@ def tile_gcgrucell_epsilon_pb_kernel(tc, x, h_dn, xg1, xg2, adj, W_u, b_u, W_c, 
                     out=w_raw[:, g, :, WIDE_CH:K_PASS],
                     in_=rows[:, 0 : PASSES * P].rearrange("o (s c) -> o s c", s=PASSES),
                 )
+
+        def load_bias():
             nc.sync.dma_start(out=bias_rows[0:OUT_TILES, :], in_=b_u.rearrange("(r o) -> r o", o=P))
             nc.sync.dma_start(out=bias_rows[OUT_TILES:GATE_TILES, :], in_=b_c.rearrange("(r o) -> r o", o=P))
 
-        load_weights()
-        for r in range(ROUNDS):
-            if r < BATCH:
-                load_batch(r)
-            if r >= GATE_LAG:
-                load_h_rows(r - GATE_LAG)
+        load_xg2(0)
+        load_h2()
+        nc.sync.dma_start(out=adj_raw[:], in_=adj.rearrange("(c w) v -> w c v", w=P))
+        load_xg1(0)
+        load_xg2(1)
+        load_xg1(1)
 
         def k_onto_partitions(sources, grouped, copy):
             turned = psum.tile([P, 2, 2, P], F32, tag="bank")
@@ -134,8 +143,8 @@ def tile_gcgrucell_epsilon_pb_kernel(tc, x, h_dn, xg1, xg2, adj, W_u, b_u, W_c, 
             return grouped
 
         def quantise_turned_xg2(grouped):
-            codes = work.tile([P, PACK, P], U32, name="hop_codes", align_bytes=64)
-            scales = work.tile([P, PACK, P], U8, name="hop_scales", align_bytes=64)
+            codes = batches.tile([P, PACK, P], U32, name="hop_codes", align_bytes=64)
+            scales = batches.tile([P, PACK, P], U8, name="hop_scales", align_bytes=64)
             nc.vector.quantize_mx(
                 out=codes[:].rearrange("p j m -> p (j m)").bitcast(FP8X4),
                 scales=scales[:].rearrange("p j m -> p (j m)"),
@@ -147,23 +156,18 @@ def tile_gcgrucell_epsilon_pb_kernel(tc, x, h_dn, xg1, xg2, adj, W_u, b_u, W_c, 
         w_codes = const.tile([P, PASSES, GATE_TILES, P], U32, align_bytes=64)
         w_scales = const.tile([P, PASSES, GATE_TILES, P], U8, align_bytes=64)
 
-        def quantise_weights():
-            banks = [(g, s) for g in range(0, GATE_TILES, 2) for s in range(PASSES)]
-            for i in range(len(banks) + 1):
-                if i < len(banks):
-                    g, s = banks[i]
-                    k_onto_partitions(
-                        [w_raw[:, g, s, :], w_raw[:, g + 1, s, :]],
-                        w_grouped[:, s, g : g + 2],
-                        (nc.scalar.copy, nc.vector.tensor_copy)[i % 2],
-                    )
-                if i > 0:
-                    g, s = banks[i - 1]
-                    nc.vector.quantize_mx(
-                        out=w_codes[:, s, g : g + 2].rearrange("p g o -> p (g o)").bitcast(FP8X4),
-                        scales=w_scales[:, s, g : g + 2].rearrange("p g o -> p (g o)"),
-                        in_=w_grouped[:, s, g : g + 2].rearrange("p g o t -> p (g o t)"),
-                    )
+        def turn_weights(s):
+            for g in range(0, GATE_TILES, 2):
+                k_onto_partitions(
+                    [w_raw[:, g, s, :], w_raw[:, g + 1, s, :]], w_grouped[:, s, g : g + 2], nc.scalar.copy
+                )
+
+        def quantise_weights(s):
+            nc.vector.quantize_mx(
+                out=w_codes[:, s].rearrange("p g o -> p (g o)").bitcast(FP8X4),
+                scales=w_scales[:, s].rearrange("p g o -> p (g o)"),
+                in_=w_grouped[:, s].rearrange("p g o t -> p (g o t)"),
+            )
 
         bias = const.tile([P, GATE_TILES], F32)
 
@@ -179,8 +183,8 @@ def tile_gcgrucell_epsilon_pb_kernel(tc, x, h_dn, xg1, xg2, adj, W_u, b_u, W_c, 
             )
 
         def quantise_loaded_passes(grouped):
-            codes = ahead.tile([P, 2, NODES], U32, name="z01_codes", align_bytes=64)
-            scales = ahead.tile([P, 2, NODES], U8, name="z01_scales", align_bytes=64)
+            codes = batches.tile([P, 2, NODES], U32, name="z01_codes", align_bytes=64)
+            scales = batches.tile([P, 2, NODES], U8, name="z01_scales", align_bytes=64)
             nc.vector.quantize_mx(
                 out=codes[:].rearrange("p s n -> p (s n)").bitcast(FP8X4),
                 scales=scales[:].rearrange("p s n -> p (s n)"),
@@ -214,8 +218,8 @@ def tile_gcgrucell_epsilon_pb_kernel(tc, x, h_dn, xg1, xg2, adj, W_u, b_u, W_c, 
                 )
 
         def quantise_hop_pass(z2_grouped):
-            codes = ahead.tile([P, NODES], U32, name="z2_codes", align_bytes=64)
-            scales = ahead.tile([P, NODES], U8, name="z2_scales", align_bytes=64)
+            codes = batches.tile([P, NODES], U32, name="z2_codes", align_bytes=64)
+            scales = batches.tile([P, NODES], U8, name="z2_scales", align_bytes=64)
             nc.vector.quantize_mx(
                 out=codes[:].bitcast(FP8X4),
                 scales=scales[:],
@@ -241,7 +245,7 @@ def tile_gcgrucell_epsilon_pb_kernel(tc, x, h_dn, xg1, xg2, adj, W_u, b_u, W_c, 
             return sums
 
         def gate_functions(sums):
-            gate = deep.tile([P, GATE_TILES, NODES], F32, name="gate")
+            gate = batches.tile([P, GATE_TILES, NODES], F32, name="gate")
             for g in GATE_ORDER:
                 nc.scalar.activation(
                     out=gate[:, g, :],
@@ -252,48 +256,128 @@ def tile_gcgrucell_epsilon_pb_kernel(tc, x, h_dn, xg1, xg2, adj, W_u, b_u, W_c, 
                 )
             return gate
 
-        def blend(b, gate):
-            update, candidate = gate[:, 0:OUT_TILES], gate[:, OUT_TILES:GATE_TILES]
-            mixed = work.tile([P, OUT_TILES, NODES], F32, name="mixed")
-            for t in range(OUT_TILES):
-                nc.vector.tensor_tensor(out=mixed[:, t], in0=h_rows[b][:, t], in1=candidate[:, t], op=ALU.subtract)
-            for t in range(OUT_TILES):
-                nc.vector.tensor_tensor(out=mixed[:, t], in0=mixed[:, t], in1=update[:, t], op=ALU.mult)
-            for t in range(OUT_TILES):
-                nc.vector.tensor_tensor(out=mixed[:, t], in0=mixed[:, t], in1=candidate[:, t], op=ALU.add)
-                nc.sync.dma_start(out=out[b, t * P : (t + 1) * P, :], in_=mixed[:, t])
+        mixed = {}
 
-        hop_operands, z2_grouped, z01, z2 = {}, {}, {}, {}
+        def blend_difference(b, t):
+            if b not in mixed:
+                mixed[b] = batches.tile([P, OUT_TILES, NODES], F32, name="mixed")
+            candidate = gate[b][:, OUT_TILES:GATE_TILES]
+            nc.vector.tensor_tensor(out=mixed[b][:, t], in0=h_rows[b][:, t], in1=candidate[:, t], op=ALU.subtract)
 
-        quantise_weights()
+        def blend_product(b, t):
+            update = gate[b][:, 0:OUT_TILES]
+            nc.vector.tensor_tensor(out=mixed[b][:, t], in0=mixed[b][:, t], in1=update[:, t], op=ALU.mult)
+
+        def blend_sum(b, t):
+            candidate = gate[b][:, OUT_TILES:GATE_TILES]
+            nc.vector.tensor_tensor(out=mixed[b][:, t], in0=mixed[b][:, t], in1=candidate[:, t], op=ALU.add)
+            rows = out[b].rearrange("(t o) n -> o t n", o=P)
+            nc.sync.dma_start(out=rows[:, t], in_=mixed[b][:, t])
+
+        hop_grouped, hop_operands, hop_banks, z01_grouped, z01, z2 = {}, {}, {}, {}, {}, {}
+
+        def turn(b):
+            hop_grouped[b] = turn_xg2(b)
+
+        def hop(b):
+            round_hop(hop_products(*hop_operands[b]), z2_grouped[b])
+
+        def regroup_xg2(b):
+            z01_grouped[b] = batches.tile([P, 2, NODES, PACK], BF16, name="z01_grouped", align_bytes=64)
+            side_by_side(nc.vector.tensor_copy, z01_grouped[b][:, 1], raw_xg2[b][:])
+
+        def regroup_xg1(b, copy, nodes=slice(0, NODES)):
+            side_by_side(copy, z01_grouped[b][:, 0, nodes], raw_xg1[b][:, :, nodes])
+
+        def quantise_hop_operand(b):
+            hop_operands[b] = quantise_turned_xg2(hop_grouped[b])
+
+        def quantise_z01(b):
+            z01[b] = quantise_loaded_passes(z01_grouped[b])
+
+        def quantise_z2(b):
+            z2[b] = quantise_hop_pass(z2_grouped[b])
+
+        gate = {}
+
+        def gates(b):
+            sums = gate_sums(
+                [
+                    (z01[b][0][:, 0, :], z01[b][1][:, 0, :]),
+                    (z01[b][0][:, 1, :], z01[b][1][:, 1, :]),
+                    (z2[b][0][:], z2[b][1][:]),
+                ]
+            )
+            gate[b] = gate_functions(sums)
+
+        both = slice(0, OUT_TILES)
+        low, high = slice(0, NODES // 2), slice(NODES // 2, NODES)
+        for b in range(BATCH):
+            z2_grouped[b] = batches.tile([P, NODES, PACK], BF16, name="z2_grouped", align_bytes=64)
+
+        turn(0)
+        regroup_xg2(0)
+        side_by_side(nc.vector.tensor_copy, h2_grouped[:], h2_raw[:])
+        for b in range(BATCH):
+            move_h2(b)
+        load_xg2(2)
+        load_weights()
+        load_bias()
+        load_xg1(2)
+        load_xg2(3)
+        load_xg1(3)
+        for b in range(BATCH):
+            load_h_rows(b)
+        quantise_hop_operand(0)
+        turn_adj()
+        quantise_adj()
+        regroup_xg1(0, nc.scalar.copy)
+        regroup_xg2(1)
+        turn(1)
+        hop(0)
+        quantise_z01(0)
+        quantise_hop_operand(1)
+        for s in range(PASSES):
+            turn_weights(s)
+        regroup_xg1(1, nc.vector.tensor_copy)
+        quantise_z01(1)
+        quantise_z2(0)
+        regroup_xg2(2)
+        quantise_weights(0)
+        quantise_weights(1)
+        quantise_weights(2)
         spread_bias()
-        for r in range(ROUNDS):
-            new, hopped, done = r, r - 1, r - GATE_LAG
-            if new < BATCH:
-                hop_grouped = turn_xg2(new)
-                if new == 0:
-                    turn_adj()
-            if 0 <= hopped < BATCH:
-                round_hop(hop_products(*hop_operands[hopped]), z2_grouped[hopped])
-            if new < BATCH:
-                z2_grouped[new] = deep.tile([P, NODES, PACK], BF16, name="z2_grouped", align_bytes=64)
-                side_by_side(nc.scalar.copy, z2_grouped[new][WIDE_PARTS:P], raw_xg3[new][WIDE_PARTS:P])
-            if new < BATCH:
-                z01_grouped = work.tile([P, 2, NODES, PACK], BF16, name="z01_grouped", align_bytes=64)
-                side_by_side(nc.vector.tensor_copy, z01_grouped[:, 1], raw_xg2[new][:])
-                hop_operands[new] = quantise_turned_xg2(hop_grouped)
-                side_by_side(nc.vector.tensor_copy, z01_grouped[:, 0], raw_xg1[new][:])
-                if new == 0:
-                    quantise_adj()
-                z01[new] = quantise_loaded_passes(z01_grouped)
-            if 0 <= hopped < BATCH:
-                z2[hopped] = quantise_hop_pass(z2_grouped[hopped])
-            if done >= 0:
-                sums = gate_sums(
-                    [
-                        (z01[done][0][:, 0, :], z01[done][1][:, 0, :]),
-                        (z01[done][0][:, 1, :], z01[done][1][:, 1, :]),
-                        (z2[done][0][:], z2[done][1][:]),
-                    ]
-                )
-                blend(done, gate_functions(sums))
+        turn(2)
+        hop(1)
+        gates(0)
+        regroup_xg1(2, nc.vector.tensor_copy)
+        quantise_hop_operand(2)
+        quantise_z01(2)
+        quantise_z2(1)
+        turn(3)
+        hop(2)
+        regroup_xg2(3)
+        blend_difference(0, both)
+        gates(1)
+        quantise_hop_operand(3)
+        blend_product(0, both)
+        regroup_xg1(3, nc.vector.tensor_copy)
+        blend_sum(0, both)
+        quantise_z2(2)
+        hop(3)
+        gates(2)
+        quantise_z01(3)
+        blend_difference(1, both)
+        quantise_z2(3)
+        gates(3)
+        blend_product(1, both)
+        blend_difference(2, both)
+        blend_sum(1, both)
+        blend_product(2, both)
+        blend_difference(3, 0)
+        blend_difference(3, 1)
+        blend_sum(2, both)
+        blend_product(3, 0)
+        blend_product(3, 1)
+        blend_sum(3, 0)
+        blend_sum(3, 1)

@@ -24,6 +24,8 @@ OUT_TILES = 2
 GATE_TILES = 2 * OUT_TILES
 PASSES = 3
 PSUM_BANKS = 8
+ALTERNATE = "r (p u) -> r u p"
+HALVES = "r (u p) -> r u p"
 GATE_ORDER = (2, 3, 0, 1)
 
 FLOPS = 2 * BATCH * WIDE_CH * NODES * NODES + 2 * 2 * BATCH * OUT_TILES * P * PASSES * K_PASS * NODES
@@ -48,6 +50,14 @@ def tile_gcgrucell_epsilon_pb_kernel(tc, x, h_dn, xg1, xg2, adj, W_u, b_u, W_c, 
         nc.vector.memset(warm[:], 0.0)
         nc.scalar.activation(out=warm[:], in_=warm[:], func=ACT.Sigmoid)
 
+        zeros = const.tile([P, NODES], BF16)
+        nc.vector.memset(zeros[:], 0.0)
+
+        def keep_tensor_busy(passes):
+            idle = psum.tile([P, NODES], F32, name="idle", tag="bank")
+            for i in range(passes):
+                nc.tensor.matmul(idle[:], lhsT=zeros[:, 0:P], rhs=zeros[:], start=True, stop=True)
+
         def four_rows_a_partition(rows):
             return rows.rearrange("(p j) n -> p j n", j=PACK)
 
@@ -60,23 +70,20 @@ def tile_gcgrucell_epsilon_pb_kernel(tc, x, h_dn, xg1, xg2, adj, W_u, b_u, W_c, 
             return raw
 
         raw_xg1, raw_xg2, h_rows, z2_grouped = {}, {}, {}, {}
-        h2_raw = const.tile([P, PACK, NODES], BF16)
-        h2_grouped = const.tile([P, NODES, PACK], BF16)
+        x_raw = const.tile([P, PACK, NODES], BF16)
+        both = slice(0, OUT_TILES)
+        for b in range(BATCH):
+            z2_grouped[b] = batches.tile([P, NODES, PACK], BF16, name="z2_grouped", align_bytes=64)
+        x_grouped = z2_grouped[BATCH - 1]
 
-        def load_h2():
-            for b in range(BATCH):
-                nc.sync.dma_start(
-                    out=h2_raw[b * QUADRANT : (b + 1) * QUADRANT], in_=four_rows_a_partition(h_dn[b, P : 2 * P])
-                )
-
-        def move_h2(b):
-            nc.sync.dma_start(out=z2_grouped[b][WIDE_PARTS:P], in_=h2_grouped[b * QUADRANT : (b + 1) * QUADRANT])
+        def move_x(b):
+            nc.sync.dma_start(out=z2_grouped[b][WIDE_PARTS:P], in_=x_grouped[b * QUADRANT : (b + 1) * QUADRANT])
 
         def load_xg2(b):
-            raw_xg2[b] = load_pass("raw_xg2", b, xg2[b], h_dn[b, 0:P])
+            raw_xg2[b] = load_pass("raw_xg2", b, xg2[b], h_dn[b, P : 2 * P])
 
         def load_xg1(b):
-            raw_xg1[b] = load_pass("raw_xg1", b, xg1[b], x[b])
+            raw_xg1[b] = load_pass("raw_xg1", b, xg1[b], h_dn[b, 0:P])
 
         def load_h_rows(b):
             h_rows[b] = inputs.tile([P, OUT_TILES, NODES], BF16, name="h_rows_%d" % b)
@@ -87,34 +94,39 @@ def tile_gcgrucell_epsilon_pb_kernel(tc, x, h_dn, xg1, xg2, adj, W_u, b_u, W_c, 
         bias_rows = const.tile([P, P], BF16)
         nc.vector.memset(bias_rows[:], 0.0)
 
-        def load_weights():
-            for g in range(GATE_TILES):
-                weight = (W_u, W_c)[g // OUT_TILES]
-                rows = weight[(g % OUT_TILES) * P : (g % OUT_TILES + 1) * P, :]
+        def load_weights(weight, g):
+            for t in range(OUT_TILES):
+                rows = weight[t * P : (t + 1) * P, :]
                 nc.sync.dma_start(
-                    out=w_raw[:, g, :, 0:WIDE_CH],
+                    out=w_raw[:, g + t, :, 0:WIDE_CH],
                     in_=rows[:, PASSES * P :].rearrange("o (s c) -> o s c", s=PASSES),
                 )
                 nc.sync.dma_start(
-                    out=w_raw[:, g, :, WIDE_CH:K_PASS],
-                    in_=rows[:, 0 : PASSES * P].rearrange("o (s c) -> o s c", s=PASSES),
+                    out=w_raw[:, g + t, 0 : PASSES - 1, WIDE_CH:K_PASS],
+                    in_=rows[:, P : PASSES * P].rearrange("o (s c) -> o s c", c=P),
                 )
+            nc.sync.dma_start(
+                out=w_raw[:, g : g + OUT_TILES, PASSES - 1, WIDE_CH:K_PASS],
+                in_=weight[:, 0:P].rearrange("(t o) c -> o t c", o=P),
+            )
 
         def load_bias():
             nc.sync.dma_start(out=bias_rows[0:OUT_TILES, :], in_=b_u.rearrange("(r o) -> r o", o=P))
             nc.sync.dma_start(out=bias_rows[OUT_TILES:GATE_TILES, :], in_=b_c.rearrange("(r o) -> r o", o=P))
 
+        nc.sync.dma_start(out=x_raw[:], in_=four_rows_a_partition(x.rearrange("b c n -> (b c) n")))
         load_xg2(0)
-        load_h2()
         nc.sync.dma_start(out=adj_raw[:], in_=adj.rearrange("(c w) v -> w c v", w=P))
         load_xg1(0)
+        load_bias()
+        load_weights(W_c, OUT_TILES)
         load_xg2(1)
-        load_xg1(1)
+        load_weights(W_u, 0)
 
-        def k_onto_partitions(sources, grouped, copy):
+        def k_onto_partitions(sources, grouped, copy, word_order):
             turned = psum.tile([P, 2, 2, P], F32, tag="bank")
             for a in range(2):
-                words = sources[a].bitcast(F32).rearrange("r (p u) -> r u p", u=2)
+                words = sources[a].bitcast(F32).rearrange(word_order, u=2)
                 for u in range(2):
                     nc.tensor.transpose(turned[:, a, u, :], words[:, u, :], ident_f32[:])
             copy(out=grouped.bitcast(F32), in_=turned[:].rearrange("p a u r -> p a r u"))
@@ -125,7 +137,7 @@ def tile_gcgrucell_epsilon_pb_kernel(tc, x, h_dn, xg1, xg2, adj, W_u, b_u, W_c, 
 
         def turn_adj():
             for c in range(0, NODE_CHUNKS, 2):
-                k_onto_partitions([adj_raw[:, c, :], adj_raw[:, c + 1, :]], adj_grouped[:, c : c + 2], nc.scalar.copy)
+                k_onto_partitions([adj_raw[:, c, :], adj_raw[:, c + 1, :]], adj_grouped[:, c : c + 2], nc.scalar.copy, HALVES)
 
         def quantise_adj():
             nc.vector.quantize_mx(
@@ -138,7 +150,7 @@ def tile_gcgrucell_epsilon_pb_kernel(tc, x, h_dn, xg1, xg2, adj, W_u, b_u, W_c, 
             grouped = work.tile([P, PACK, P, PACK], BF16, name="hop_grouped", align_bytes=64)
             for j in range(0, PACK, 2):
                 k_onto_partitions(
-                    [raw_xg2[b][:, j, :], raw_xg2[b][:, j + 1, :]], grouped[:, j : j + 2], nc.scalar.copy
+                    [raw_xg2[b][:, j, :], raw_xg2[b][:, j + 1, :]], grouped[:, j : j + 2], nc.scalar.copy, HALVES
                 )
             return grouped
 
@@ -152,22 +164,23 @@ def tile_gcgrucell_epsilon_pb_kernel(tc, x, h_dn, xg1, xg2, adj, W_u, b_u, W_c, 
             )
             return codes, scales
 
-        w_grouped = const.tile([P, PASSES, GATE_TILES, P, PACK], BF16, align_bytes=64)
-        w_codes = const.tile([P, PASSES, GATE_TILES, P], U32, align_bytes=64)
-        w_scales = const.tile([P, PASSES, GATE_TILES, P], U8, align_bytes=64)
+        w_grouped = const.tile([P, 2, PASSES, OUT_TILES, P, PACK], BF16, align_bytes=64)
+        w_codes = const.tile([P, 2, PASSES, OUT_TILES, P], U32, align_bytes=64)
+        w_scales = const.tile([P, 2, PASSES, OUT_TILES, P], U8, align_bytes=64)
 
-        def turn_weights(s):
-            for g in range(0, GATE_TILES, 2):
+        def turn_weights(g):
+            for s in range(PASSES):
                 k_onto_partitions(
-                    [w_raw[:, g, s, :], w_raw[:, g + 1, s, :]], w_grouped[:, s, g : g + 2], nc.scalar.copy
+                    [w_raw[:, g, s, :], w_raw[:, g + 1, s, :]], w_grouped[:, g // 2, s], nc.scalar.copy, ALTERNATE
                 )
 
-        def quantise_weights(s):
-            nc.vector.quantize_mx(
-                out=w_codes[:, s].rearrange("p g o -> p (g o)").bitcast(FP8X4),
-                scales=w_scales[:, s].rearrange("p g o -> p (g o)"),
-                in_=w_grouped[:, s].rearrange("p g o t -> p (g o t)"),
-            )
+        def quantise_weights(g):
+            for s in (slice(0, 2), slice(2, PASSES)):
+                nc.vector.quantize_mx(
+                    out=w_codes[:, g // 2, s].rearrange("p s g o -> p (s g o)").bitcast(FP8X4),
+                    scales=w_scales[:, g // 2, s].rearrange("p s g o -> p (s g o)"),
+                    in_=w_grouped[:, g // 2, s].rearrange("p s g o t -> p (s g o t)"),
+                )
 
         bias = const.tile([P, GATE_TILES], F32)
 
@@ -235,8 +248,8 @@ def tile_gcgrucell_epsilon_pb_kernel(tc, x, h_dn, xg1, xg2, adj, W_u, b_u, W_c, 
                     z_codes, z_scales = z_operands[s]
                     nc.tensor.matmul_mx(
                         out=sums[g][:],
-                        lhsT=w_codes[:, s, g, :].bitcast(FP8X4),
-                        lhsT_scale=w_scales[:, s, g, :],
+                        lhsT=w_codes[:, g // OUT_TILES, s, g % OUT_TILES, :].bitcast(FP8X4),
+                        lhsT_scale=w_scales[:, g // OUT_TILES, s, g % OUT_TILES, :],
                         rhs=z_codes.bitcast(FP8X4),
                         rhs_scale=z_scales,
                         start=(s == 0),
@@ -312,71 +325,76 @@ def tile_gcgrucell_epsilon_pb_kernel(tc, x, h_dn, xg1, xg2, adj, W_u, b_u, W_c, 
 
         both = slice(0, OUT_TILES)
         low, high = slice(0, NODES // 2), slice(NODES // 2, NODES)
-        for b in range(BATCH):
-            z2_grouped[b] = batches.tile([P, NODES, PACK], BF16, name="z2_grouped", align_bytes=64)
-
-        turn(0)
-        regroup_xg2(0)
-        side_by_side(nc.vector.tensor_copy, h2_grouped[:], h2_raw[:])
-        for b in range(BATCH):
-            move_h2(b)
+        keep_tensor_busy(6)
+        side_by_side(nc.vector.tensor_copy, x_grouped[:], x_raw[:])
+        move_x(0)
+        load_xg1(1)
         load_xg2(2)
-        load_weights()
-        load_bias()
+        move_x(1)
+        load_h_rows(0)
         load_xg1(2)
         load_xg2(3)
+        move_x(2)
         load_xg1(3)
-        for b in range(BATCH):
-            load_h_rows(b)
+        load_h_rows(1)
+        load_h_rows(2)
+        load_h_rows(3)
+        turn(0)
+        keep_tensor_busy(2)
+        regroup_xg2(0)
         quantise_hop_operand(0)
+        regroup_xg1(0, nc.vector.tensor_copy, low)
         turn_adj()
+        keep_tensor_busy(2)
+        regroup_xg1(0, nc.scalar.copy, high)
         quantise_adj()
-        regroup_xg1(0, nc.scalar.copy)
-        regroup_xg2(1)
-        turn(1)
         hop(0)
         quantise_z01(0)
-        quantise_hop_operand(1)
-        for s in range(PASSES):
-            turn_weights(s)
-        regroup_xg1(1, nc.vector.tensor_copy)
-        quantise_z01(1)
-        quantise_z2(0)
-        regroup_xg2(2)
-        quantise_weights(0)
-        quantise_weights(1)
-        quantise_weights(2)
         spread_bias()
-        turn(2)
+        turn_weights(OUT_TILES)
+        keep_tensor_busy(2)
+        regroup_xg2(1)
+        turn(1)
+        keep_tensor_busy(2)
+        quantise_weights(OUT_TILES)
+        quantise_z2(0)
+        quantise_hop_operand(1)
+        turn_weights(0)
+        quantise_weights(0)
         hop(1)
+        regroup_xg1(1, nc.vector.tensor_copy)
         gates(0)
-        regroup_xg1(2, nc.vector.tensor_copy)
-        quantise_hop_operand(2)
-        quantise_z01(2)
+        quantise_z01(1)
+        turn(2)
+        regroup_xg2(2)
         quantise_z2(1)
+        gates(1)
+        blend_difference(0, both)
+        quantise_hop_operand(2)
+        blend_product(0, both)
         turn(3)
         hop(2)
-        regroup_xg2(3)
-        blend_difference(0, both)
-        gates(1)
-        quantise_hop_operand(3)
-        blend_product(0, both)
-        regroup_xg1(3, nc.vector.tensor_copy)
+        regroup_xg1(2, nc.vector.tensor_copy)
         blend_sum(0, both)
+        quantise_z01(2)
+        regroup_xg2(3)
+        quantise_hop_operand(3)
         quantise_z2(2)
+        regroup_xg1(3, nc.scalar.copy, high)
         hop(3)
         gates(2)
-        quantise_z01(3)
         blend_difference(1, both)
+        regroup_xg1(3, nc.vector.tensor_copy, low)
+        blend_product(1, both)
+        quantise_z01(3)
         quantise_z2(3)
         gates(3)
-        blend_product(1, both)
-        blend_difference(2, both)
         blend_sum(1, both)
+        blend_difference(2, both)
         blend_product(2, both)
         blend_difference(3, 0)
-        blend_difference(3, 1)
         blend_sum(2, both)
+        blend_difference(3, 1)
         blend_product(3, 0)
         blend_product(3, 1)
         blend_sum(3, 0)

@@ -23,6 +23,7 @@ QUADRANT = 32
 OUT_TILES = 2
 GATE_TILES = 2 * OUT_TILES
 PASSES = 3
+Z_CH = PASSES * K_PASS
 PSUM_BANKS = 8
 ALTERNATE = "r (p u) -> r u p"
 HALVES = "r (u p) -> r u p"
@@ -61,12 +62,10 @@ def tile_gcgrucell_epsilon_pb_kernel(tc, x, h_dn, xg1, xg2, adj, W_u, b_u, W_c, 
         def four_rows_a_partition(rows):
             return rows.rearrange("(p j) n -> p j n", j=PACK)
 
-        def load_pass(name, b, wide, narrow):
+        def load_pass(name, b, parts):
             raw = inputs.tile([P, PACK, NODES], BF16, name="%s_%d" % (name, b))
-            if wide is not None:
-                nc.sync.dma_start(out=raw[QUADRANT:WIDE_PARTS], in_=four_rows_a_partition(wide[PACK * QUADRANT :]))
-                nc.sync.dma_start(out=raw[0:QUADRANT], in_=four_rows_a_partition(wide[0 : PACK * QUADRANT]))
-            nc.sync.dma_start(out=raw[WIDE_PARTS:P], in_=four_rows_a_partition(narrow))
+            for first, rows in parts:
+                nc.sync.dma_start(out=raw[first : first + rows.shape[0] // PACK], in_=four_rows_a_partition(rows))
             return raw
 
         raw_xg1, raw_xg2, h_rows, z2_grouped = {}, {}, {}, {}
@@ -80,35 +79,32 @@ def tile_gcgrucell_epsilon_pb_kernel(tc, x, h_dn, xg1, xg2, adj, W_u, b_u, W_c, 
             nc.sync.dma_start(out=z2_grouped[b][WIDE_PARTS:P], in_=x_grouped[b * QUADRANT : (b + 1) * QUADRANT])
 
         def load_xg2(b):
-            raw_xg2[b] = load_pass("raw_xg2", b, xg2[b], h_dn[b, P : 2 * P])
+            raw_xg2[b] = load_pass(
+                "raw_xg2", b, [(QUADRANT, xg2[b, P:WIDE_CH]), (0, xg2[b, 0:P]), (WIDE_PARTS, h_dn[b, 0:P])]
+            )
 
         def load_xg1(b):
-            raw_xg1[b] = load_pass("raw_xg1", b, xg1[b], h_dn[b, 0:P])
+            raw_xg1[b] = load_pass(
+                "raw_xg1", b, [(QUADRANT, xg1[b, 0 : 2 * P]), (WIDE_PARTS, xg1[b, 2 * P :]), (0, h_dn[b, P : 2 * P])]
+            )
 
         def load_h_rows(b):
             h_rows[b] = inputs.tile([P, OUT_TILES, NODES], BF16, name="h_rows_%d" % b)
             nc.sync.dma_start(out=h_rows[b][:], in_=h_dn[b].rearrange("(t o) n -> o t n", o=P))
 
         adj_raw = const.tile([P, NODE_CHUNKS, NODES], BF16)
-        w_raw = const.tile([P, GATE_TILES, PASSES, K_PASS], BF16)
+        w_raw = const.tile([P, GATE_TILES, Z_CH], BF16)
         bias_rows = const.tile([P, P], BF16)
         nc.vector.memset(bias_rows[:], 0.0)
 
         def load_weights(weight, g):
-            for t in range(OUT_TILES):
-                rows = weight[t * P : (t + 1) * P, :]
+            rows = weight.rearrange("(t o) k -> o t k", o=P)
+            to = 0
+            for first, end in ((2 * P, 3 * P + 2 * WIDE_CH), (P, 2 * P), (3 * P + 2 * WIDE_CH, Z_CH), (0, P)):
                 nc.sync.dma_start(
-                    out=w_raw[:, g + t, :, 0:WIDE_CH],
-                    in_=rows[:, PASSES * P :].rearrange("o (s c) -> o s c", s=PASSES),
+                    out=w_raw[:, g : g + OUT_TILES, to : to + end - first], in_=rows[:, :, first:end]
                 )
-                nc.sync.dma_start(
-                    out=w_raw[:, g + t, 0 : PASSES - 1, WIDE_CH:K_PASS],
-                    in_=rows[:, P : PASSES * P].rearrange("o (s c) -> o s c", c=P),
-                )
-            nc.sync.dma_start(
-                out=w_raw[:, g : g + OUT_TILES, PASSES - 1, WIDE_CH:K_PASS],
-                in_=weight[:, 0:P].rearrange("(t o) c -> o t c", o=P),
-            )
+                to += end - first
 
         def load_bias():
             nc.sync.dma_start(out=bias_rows[0:OUT_TILES, :], in_=b_u.rearrange("(r o) -> r o", o=P))
@@ -129,7 +125,8 @@ def tile_gcgrucell_epsilon_pb_kernel(tc, x, h_dn, xg1, xg2, adj, W_u, b_u, W_c, 
                 words = sources[a].bitcast(F32).rearrange(word_order, u=2)
                 for u in range(2):
                     nc.tensor.transpose(turned[:, a, u, :], words[:, u, :], ident_f32[:])
-            copy(out=grouped.bitcast(F32), in_=turned[:].rearrange("p a u r -> p a r u"))
+            rows = grouped.shape[2]
+            copy(out=grouped.bitcast(F32), in_=turned[:, :, :, 0:rows].rearrange("p a u r -> p a r u"))
 
         adj_grouped = const.tile([P, NODE_CHUNKS, P, PACK], BF16, align_bytes=64)
         adj_codes = const.tile([P, NODES], U32, align_bytes=64)
@@ -146,11 +143,20 @@ def tile_gcgrucell_epsilon_pb_kernel(tc, x, h_dn, xg1, xg2, adj, W_u, b_u, W_c, 
                 in_=adj_grouped[:].rearrange("p c w t -> p (c w t)"),
             )
 
+        hop_grouped_tiles = []
+        for i in range(2):
+            tile = const.tile([P, PACK, P, PACK], BF16, name="hop_grouped_%d" % i, align_bytes=64)
+            nc.gpsimd.memset(tile[:, :, WIDE_PARTS:P], 0.0)
+            hop_grouped_tiles.append(tile)
+
         def turn_xg2(b):
-            grouped = work.tile([P, PACK, P, PACK], BF16, name="hop_grouped", align_bytes=64)
+            grouped = hop_grouped_tiles[b % 2]
             for j in range(0, PACK, 2):
                 k_onto_partitions(
-                    [raw_xg2[b][:, j, :], raw_xg2[b][:, j + 1, :]], grouped[:, j : j + 2], nc.scalar.copy, HALVES
+                    [raw_xg2[b][:, j, :], raw_xg2[b][:, j + 1, :]],
+                    grouped[:, j : j + 2, 0:WIDE_PARTS],
+                    nc.scalar.copy,
+                    HALVES,
                 )
             return grouped
 
@@ -171,7 +177,7 @@ def tile_gcgrucell_epsilon_pb_kernel(tc, x, h_dn, xg1, xg2, adj, W_u, b_u, W_c, 
         def turn_weights(g):
             for s in range(PASSES):
                 k_onto_partitions(
-                    [w_raw[:, g, s, :], w_raw[:, g + 1, s, :]], w_grouped[:, g // 2, s], nc.scalar.copy, ALTERNATE
+                    [w_raw[:, g + t, s * K_PASS : (s + 1) * K_PASS] for t in range(OUT_TILES)], w_grouped[:, g // 2, s], nc.scalar.copy, ALTERNATE
                 )
 
         def quantise_weights(g):
@@ -257,9 +263,9 @@ def tile_gcgrucell_epsilon_pb_kernel(tc, x, h_dn, xg1, xg2, adj, W_u, b_u, W_c, 
                     )
             return sums
 
-        def gate_functions(sums):
+        def gate_functions(sums, between):
             gate = batches.tile([P, GATE_TILES, NODES], F32, name="gate")
-            for g in GATE_ORDER:
+            for i, g in enumerate(GATE_ORDER):
                 nc.scalar.activation(
                     out=gate[:, g, :],
                     in_=sums[g][:],
@@ -267,6 +273,7 @@ def tile_gcgrucell_epsilon_pb_kernel(tc, x, h_dn, xg1, xg2, adj, W_u, b_u, W_c, 
                     bias=bias[:, g : g + 1],
                     scale=1.0,
                 )
+                between(i)
             return gate
 
         mixed = {}
@@ -281,11 +288,12 @@ def tile_gcgrucell_epsilon_pb_kernel(tc, x, h_dn, xg1, xg2, adj, W_u, b_u, W_c, 
             update = gate[b][:, 0:OUT_TILES]
             nc.vector.tensor_tensor(out=mixed[b][:, t], in0=mixed[b][:, t], in1=update[:, t], op=ALU.mult)
 
-        def blend_sum(b, t):
-            candidate = gate[b][:, OUT_TILES:GATE_TILES]
-            nc.vector.tensor_tensor(out=mixed[b][:, t], in0=mixed[b][:, t], in1=candidate[:, t], op=ALU.add)
+        def blend_sum(b, t, nodes=slice(0, NODES)):
+            candidate = gate[b][:, OUT_TILES:GATE_TILES, nodes]
+            result = mixed[b][:, t, nodes]
+            nc.vector.tensor_tensor(out=result, in0=result, in1=candidate[:, t], op=ALU.add)
             rows = out[b].rearrange("(t o) n -> o t n", o=P)
-            nc.sync.dma_start(out=rows[:, t], in_=mixed[b][:, t])
+            nc.sync.dma_start(out=rows[:, t, nodes], in_=result)
 
         hop_grouped, hop_operands, hop_banks, z01_grouped, z01, z2 = {}, {}, {}, {}, {}, {}
 
@@ -313,7 +321,7 @@ def tile_gcgrucell_epsilon_pb_kernel(tc, x, h_dn, xg1, xg2, adj, W_u, b_u, W_c, 
 
         gate = {}
 
-        def gates(b):
+        def gates(b, between=lambda i: None):
             sums = gate_sums(
                 [
                     (z01[b][0][:, 0, :], z01[b][1][:, 0, :]),
@@ -321,7 +329,7 @@ def tile_gcgrucell_epsilon_pb_kernel(tc, x, h_dn, xg1, xg2, adj, W_u, b_u, W_c, 
                     (z2[b][0][:], z2[b][1][:]),
                 ]
             )
-            gate[b] = gate_functions(sums)
+            gate[b] = gate_functions(sums, between)
 
         both = slice(0, OUT_TILES)
         low, high = slice(0, NODES // 2), slice(NODES // 2, NODES)
@@ -398,4 +406,5 @@ def tile_gcgrucell_epsilon_pb_kernel(tc, x, h_dn, xg1, xg2, adj, W_u, b_u, W_c, 
         blend_product(3, 0)
         blend_product(3, 1)
         blend_sum(3, 0)
-        blend_sum(3, 1)
+        blend_sum(3, 1, low)
+        blend_sum(3, 1, high)

@@ -62,13 +62,7 @@ def tile_gcgrucell_epsilon_pb_kernel(tc, x, h_dn, xg1, xg2, adj, W_u, b_u, W_c, 
         def four_rows_a_partition(rows):
             return rows.rearrange("(p j) n -> p j n", j=PACK)
 
-        def load_pass(name, b, parts):
-            raw = inputs.tile([P, PACK, NODES], BF16, name="%s_%d" % (name, b))
-            for first, rows in parts:
-                nc.sync.dma_start(out=raw[first : first + rows.shape[0] // PACK], in_=four_rows_a_partition(rows))
-            return raw
-
-        raw_xg1, raw_xg2, h_rows, z2_grouped = {}, {}, {}, {}
+        raw_0, raw_1, xg2_rows, h_rows, z2_grouped = {}, {}, {}, {}, {}
         x_raw = const.tile([P, PACK, NODES], BF16)
         both = slice(0, OUT_TILES)
         for b in range(BATCH):
@@ -78,15 +72,18 @@ def tile_gcgrucell_epsilon_pb_kernel(tc, x, h_dn, xg1, xg2, adj, W_u, b_u, W_c, 
         def move_x(b):
             nc.sync.dma_start(out=z2_grouped[b][WIDE_PARTS:P], in_=x_grouped[b * QUADRANT : (b + 1) * QUADRANT])
 
-        def load_xg2(b):
-            raw_xg2[b] = load_pass(
-                "raw_xg2", b, [(QUADRANT, xg2[b, P:WIDE_CH]), (0, xg2[b, 0:P]), (WIDE_PARTS, h_dn[b, 0:P])]
-            )
+        def load_pass_1(b):
+            raw_1[b] = inputs.tile([P, PACK, NODES], BF16, name="raw_1_%d" % b)
+            nc.sync.dma_start(out=raw_1[b][:, 2:PACK], in_=xg2[b, 0 : 2 * P].rearrange("(p e) n -> p e n", e=2))
+            xg2_rows[b] = inputs.tile([P, NODES], BF16, name="xg2_rows_%d" % b)
+            nc.sync.dma_start(out=xg2_rows[b][:], in_=xg2[b, 2 * P : WIDE_CH])
+            nc.sync.dma_start(out=raw_1[b][:, 0:2], in_=xg1[b, P:WIDE_CH].rearrange("(p e) n -> p e n", e=2))
 
-        def load_xg1(b):
-            raw_xg1[b] = load_pass(
-                "raw_xg1", b, [(QUADRANT, xg1[b, 0 : 2 * P]), (WIDE_PARTS, xg1[b, 2 * P :]), (0, h_dn[b, P : 2 * P])]
-            )
+        def load_pass_0(b):
+            raw_0[b] = inputs.tile([P, PACK, NODES], BF16, name="raw_0_%d" % b)
+            nc.sync.dma_start(out=raw_0[b][QUADRANT:WIDE_PARTS], in_=four_rows_a_partition(h_dn[b]))
+            nc.sync.dma_start(out=raw_0[b][0:QUADRANT], in_=four_rows_a_partition(xg2[b, 2 * P : WIDE_CH]))
+            nc.sync.dma_start(out=raw_0[b][WIDE_PARTS:P], in_=four_rows_a_partition(xg1[b, 0:P]))
 
         def load_h_rows(b):
             h_rows[b] = inputs.tile([P, OUT_TILES, NODES], BF16, name="h_rows_%d" % b)
@@ -99,34 +96,41 @@ def tile_gcgrucell_epsilon_pb_kernel(tc, x, h_dn, xg1, xg2, adj, W_u, b_u, W_c, 
 
         def load_weights(weight, g):
             rows = weight.rearrange("(t o) k -> o t k", o=P)
-            to = 0
-            for first, end in ((2 * P, 3 * P + 2 * WIDE_CH), (P, 2 * P), (3 * P + 2 * WIDE_CH, Z_CH), (0, P)):
+            xg2_end = 3 * P + 2 * WIDE_CH
+            for to, first, end in (
+                (P, P, 2 * K_PASS),
+                (0, 2 * K_PASS, xg2_end),
+                (2 * K_PASS, xg2_end, Z_CH),
+                (Z_CH - P, 0, P),
+            ):
                 nc.sync.dma_start(
                     out=w_raw[:, g : g + OUT_TILES, to : to + end - first], in_=rows[:, :, first:end]
                 )
-                to += end - first
 
         def load_bias():
             nc.sync.dma_start(out=bias_rows[0:OUT_TILES, :], in_=b_u.rearrange("(r o) -> r o", o=P))
             nc.sync.dma_start(out=bias_rows[OUT_TILES:GATE_TILES, :], in_=b_c.rearrange("(r o) -> r o", o=P))
 
         nc.sync.dma_start(out=x_raw[:], in_=four_rows_a_partition(x.rearrange("b c n -> (b c) n")))
-        load_xg2(0)
+        load_pass_1(0)
         nc.sync.dma_start(out=adj_raw[:], in_=adj.rearrange("(c w) v -> w c v", w=P))
-        load_xg1(0)
+        load_pass_0(0)
         load_bias()
         load_weights(W_c, OUT_TILES)
-        load_xg2(1)
+        load_pass_1(1)
         load_weights(W_u, 0)
 
-        def k_onto_partitions(sources, grouped, copy, word_order):
+        def turn(sources, word_order):
             turned = psum.tile([P, 2, 2, P], F32, tag="bank")
-            for a in range(2):
-                words = sources[a].bitcast(F32).rearrange(word_order, u=2)
+            for a, source in enumerate(sources):
+                words = source.bitcast(F32).rearrange(word_order, u=2)
                 for u in range(2):
                     nc.tensor.transpose(turned[:, a, u, :], words[:, u, :], ident_f32[:])
-            rows = grouped.shape[2]
-            copy(out=grouped.bitcast(F32), in_=turned[:, :, :, 0:rows].rearrange("p a u r -> p a r u"))
+            return turned
+
+        def k_onto_partitions(sources, grouped, word_order):
+            turned = turn(sources, word_order)
+            nc.scalar.copy(out=grouped.bitcast(F32), in_=turned[:].rearrange("p a u r -> p a r u"))
 
         adj_grouped = const.tile([P, NODE_CHUNKS, P, PACK], BF16, align_bytes=64)
         adj_codes = const.tile([P, NODES], U32, align_bytes=64)
@@ -134,7 +138,7 @@ def tile_gcgrucell_epsilon_pb_kernel(tc, x, h_dn, xg1, xg2, adj, W_u, b_u, W_c, 
 
         def turn_adj():
             for c in range(0, NODE_CHUNKS, 2):
-                k_onto_partitions([adj_raw[:, c, :], adj_raw[:, c + 1, :]], adj_grouped[:, c : c + 2], nc.scalar.copy, HALVES)
+                k_onto_partitions([adj_raw[:, c, :], adj_raw[:, c + 1, :]], adj_grouped[:, c : c + 2], HALVES)
 
         def quantise_adj():
             nc.vector.quantize_mx(
@@ -151,13 +155,15 @@ def tile_gcgrucell_epsilon_pb_kernel(tc, x, h_dn, xg1, xg2, adj, W_u, b_u, W_c, 
 
         def turn_xg2(b):
             grouped = hop_grouped_tiles[b % 2]
-            for j in range(0, PACK, 2):
-                k_onto_partitions(
-                    [raw_xg2[b][:, j, :], raw_xg2[b][:, j + 1, :]],
-                    grouped[:, j : j + 2, 0:WIDE_PARTS],
-                    nc.scalar.copy,
-                    HALVES,
-                )
+            words = grouped[:].rearrange("p j m t -> p (j m t)").bitcast(F32).rearrange("p (j m u) -> p j m u", j=PACK, u=2)
+            turned = turn([raw_1[b][:, 2, :], raw_1[b][:, 3, :]], HALVES)
+            by_half = turned[:].rearrange("p e u (m h) -> p h e m u", h=2)
+            for h in range(2):
+                nc.scalar.copy(out=words[:, 2 * h : 2 * h + 2, 0 : P // 2], in_=by_half[:, h])
+            turned = turn([xg2_rows[b][:]], HALVES)
+            nc.scalar.copy(
+                out=words[:, :, P // 2 : WIDE_PARTS], in_=turned[:, 0].rearrange("p u (q j) -> p j q u", j=PACK)
+            )
             return grouped
 
         def quantise_turned_xg2(grouped):
@@ -177,7 +183,9 @@ def tile_gcgrucell_epsilon_pb_kernel(tc, x, h_dn, xg1, xg2, adj, W_u, b_u, W_c, 
         def turn_weights(g):
             for s in range(PASSES):
                 k_onto_partitions(
-                    [w_raw[:, g + t, s * K_PASS : (s + 1) * K_PASS] for t in range(OUT_TILES)], w_grouped[:, g // 2, s], nc.scalar.copy, ALTERNATE
+                    [w_raw[:, g + t, s * K_PASS : (s + 1) * K_PASS] for t in range(OUT_TILES)],
+                    w_grouped[:, g // 2, s],
+                    HALVES if s == 1 else ALTERNATE,
                 )
 
         def quantise_weights(g):
@@ -297,18 +305,20 @@ def tile_gcgrucell_epsilon_pb_kernel(tc, x, h_dn, xg1, xg2, adj, W_u, b_u, W_c, 
 
         hop_grouped, hop_operands, hop_banks, z01_grouped, z01, z2 = {}, {}, {}, {}, {}, {}
 
-        def turn(b):
+        def turn_hop(b):
             hop_grouped[b] = turn_xg2(b)
 
         def hop(b):
             round_hop(hop_products(*hop_operands[b]), z2_grouped[b])
 
-        def regroup_xg2(b):
+        for b in range(BATCH):
             z01_grouped[b] = batches.tile([P, 2, NODES, PACK], BF16, name="z01_grouped", align_bytes=64)
-            side_by_side(nc.vector.tensor_copy, z01_grouped[b][:, 1], raw_xg2[b][:])
+
+        def regroup_xg2(b):
+            side_by_side(nc.vector.tensor_copy, z01_grouped[b][:, 1], raw_1[b][:])
 
         def regroup_xg1(b, copy, nodes=slice(0, NODES)):
-            side_by_side(copy, z01_grouped[b][:, 0, nodes], raw_xg1[b][:, :, nodes])
+            side_by_side(copy, z01_grouped[b][:, 0, nodes], raw_0[b][:, :, nodes])
 
         def quantise_hop_operand(b):
             hop_operands[b] = quantise_turned_xg2(hop_grouped[b])
@@ -336,18 +346,18 @@ def tile_gcgrucell_epsilon_pb_kernel(tc, x, h_dn, xg1, xg2, adj, W_u, b_u, W_c, 
         keep_tensor_busy(6)
         side_by_side(nc.vector.tensor_copy, x_grouped[:], x_raw[:])
         move_x(0)
-        load_xg1(1)
-        load_xg2(2)
+        load_pass_0(1)
+        load_pass_1(2)
         move_x(1)
         load_h_rows(0)
-        load_xg1(2)
-        load_xg2(3)
+        load_pass_0(2)
+        load_pass_1(3)
         move_x(2)
-        load_xg1(3)
+        load_pass_0(3)
         load_h_rows(1)
         load_h_rows(2)
         load_h_rows(3)
-        turn(0)
+        turn_hop(0)
         keep_tensor_busy(2)
         regroup_xg2(0)
         quantise_hop_operand(0)
@@ -362,7 +372,7 @@ def tile_gcgrucell_epsilon_pb_kernel(tc, x, h_dn, xg1, xg2, adj, W_u, b_u, W_c, 
         turn_weights(OUT_TILES)
         keep_tensor_busy(2)
         regroup_xg2(1)
-        turn(1)
+        turn_hop(1)
         keep_tensor_busy(2)
         quantise_weights(OUT_TILES)
         quantise_z2(0)
@@ -373,14 +383,14 @@ def tile_gcgrucell_epsilon_pb_kernel(tc, x, h_dn, xg1, xg2, adj, W_u, b_u, W_c, 
         regroup_xg1(1, nc.vector.tensor_copy)
         gates(0)
         quantise_z01(1)
-        turn(2)
+        turn_hop(2)
         regroup_xg2(2)
         quantise_z2(1)
         gates(1)
         blend_difference(0, both)
         quantise_hop_operand(2)
         blend_product(0, both)
-        turn(3)
+        turn_hop(3)
         hop(2)
         regroup_xg1(2, nc.vector.tensor_copy)
         blend_sum(0, both)

@@ -368,17 +368,17 @@ def tile_gcgrucell_epsilon_pb_kernel(tc, x, h_dn, xg1, xg2, adj, W_u, b_u, W_c, 
         quantise_adj()
         hop(0)
         quantise_z01(0)
-        spread_bias()
-        turn_weights(OUT_TILES)
-        keep_tensor_busy(2)
         regroup_xg2(1)
         turn_hop(1)
         keep_tensor_busy(2)
+        turn_weights(OUT_TILES)
+        keep_tensor_busy(2)
+        quantise_hop_operand(1)
         quantise_weights(OUT_TILES)
         quantise_z2(0)
-        quantise_hop_operand(1)
         turn_weights(0)
         quantise_weights(0)
+        spread_bias()
         hop(1)
         regroup_xg1(1, nc.vector.tensor_copy)
         gates(0)

@@ -21,15 +21,15 @@ WIDE_CH = 384
 WIDE_PARTS = WIDE_CH // PACK
 QUADRANT = 32
 OUT_TILES = 2
-GATE_TILES = 2 * OUT_TILES
+UPDATE, CANDIDATE = 0, 1
 PASSES = 3
 Z_CH = PASSES * K_PASS
 PSUM_BANKS = 8
 ALTERNATE = "r (p u) -> r u p"
 HALVES = "r (u p) -> r u p"
-GATE_ORDER = (2, 3, 0, 1)
+GATE_ORDER = ((CANDIDATE, 0), (CANDIDATE, 1), (UPDATE, 0), (UPDATE, 1))
 
-FLOPS = 2 * BATCH * WIDE_CH * NODES * NODES + 2 * 2 * BATCH * OUT_TILES * P * PASSES * K_PASS * NODES
+FLOPS = 2 * BATCH * WIDE_CH * NODES * NODES + 2 * 2 * BATCH * OUT_TILES * P * Z_CH * NODES
 
 
 def tile_gcgrucell_epsilon_pb_kernel(tc, x, h_dn, xg1, xg2, adj, W_u, b_u, W_c, b_c, out):
@@ -39,13 +39,10 @@ def tile_gcgrucell_epsilon_pb_kernel(tc, x, h_dn, xg1, xg2, adj, W_u, b_u, W_c, 
         const = ctx.enter_context(tc.tile_pool(name="const", bufs=1))
         inputs = ctx.enter_context(tc.tile_pool(name="inputs", bufs=1))
         batches = ctx.enter_context(tc.tile_pool(name="batches", bufs=BATCH))
-        work = ctx.enter_context(tc.tile_pool(name="work", bufs=2))
         psum = ctx.enter_context(tc.psum_pool(name="psum", bufs=PSUM_BANKS))
 
-        ident_f32 = const.tile([P, P], F32)
-        make_identity(nc, ident_f32[:])
-        ident_bf16 = const.tile([P, P], BF16)
-        make_identity(nc, ident_bf16[:])
+        identity = const.tile([P, P], F32)
+        make_identity(nc, identity[:])
 
         warm = const.tile([P, 1], F32)
         nc.vector.memset(warm[:], 0.0)
@@ -62,74 +59,78 @@ def tile_gcgrucell_epsilon_pb_kernel(tc, x, h_dn, xg1, xg2, adj, W_u, b_u, W_c, 
         def four_rows_a_partition(rows):
             return rows.rearrange("(p j) n -> p j n", j=PACK)
 
-        raw_0, raw_1, xg2_rows, h_rows, z2_grouped = {}, {}, {}, {}, {}
-        x_raw = const.tile([P, PACK, NODES], BF16)
-        both = slice(0, OUT_TILES)
-        for b in range(BATCH):
-            z2_grouped[b] = batches.tile([P, NODES, PACK], BF16, name="z2_grouped", align_bytes=64)
-        x_grouped = z2_grouped[BATCH - 1]
+        def two_rows_a_partition(rows):
+            return rows.rearrange("(p e) n -> p e n", e=2)
+
+        pass_0_rows, pass_1_rows, xg2_rows, h_rows = [], [], [], []
+        x_rows = const.tile([P, PACK, NODES], BF16)
+        pass_01_words = [
+            batches.tile([P, 2, NODES, PACK], BF16, name="pass_01_words", align_bytes=64) for b in range(BATCH)
+        ]
+        pass_2_words = [batches.tile([P, NODES, PACK], BF16, name="pass_2_words", align_bytes=64) for b in range(BATCH)]
+        x_words = pass_2_words[BATCH - 1]
+
+        def load_x():
+            nc.sync.dma_start(out=x_rows[:], in_=four_rows_a_partition(x.rearrange("b c n -> (b c) n")))
 
         def move_x(b):
-            nc.sync.dma_start(out=z2_grouped[b][WIDE_PARTS:P], in_=x_grouped[b * QUADRANT : (b + 1) * QUADRANT])
+            nc.sync.dma_start(out=pass_2_words[b][WIDE_PARTS:P], in_=x_words[b * QUADRANT : (b + 1) * QUADRANT])
 
         def load_pass_1(b):
-            raw_1[b] = inputs.tile([P, PACK, NODES], BF16, name="raw_1_%d" % b)
-            nc.sync.dma_start(out=raw_1[b][:, 2:PACK], in_=xg2[b, 0 : 2 * P].rearrange("(p e) n -> p e n", e=2))
-            xg2_rows[b] = inputs.tile([P, NODES], BF16, name="xg2_rows_%d" % b)
-            nc.sync.dma_start(out=xg2_rows[b][:], in_=xg2[b, 2 * P : WIDE_CH])
-            nc.sync.dma_start(out=raw_1[b][:, 0:2], in_=xg1[b, P:WIDE_CH].rearrange("(p e) n -> p e n", e=2))
+            rows = inputs.tile([P, PACK, NODES], BF16, name="pass_1_rows_%d" % b)
+            nc.sync.dma_start(out=rows[:, 2:PACK], in_=two_rows_a_partition(xg2[b, 0 : 2 * P]))
+            last_third = inputs.tile([P, NODES], BF16, name="xg2_rows_%d" % b)
+            nc.sync.dma_start(out=last_third[:], in_=xg2[b, 2 * P : WIDE_CH])
+            nc.sync.dma_start(out=rows[:, 0:2], in_=two_rows_a_partition(xg1[b, P:WIDE_CH]))
+            pass_1_rows.append(rows)
+            xg2_rows.append(last_third)
 
         def load_pass_0(b):
-            raw_0[b] = inputs.tile([P, PACK, NODES], BF16, name="raw_0_%d" % b)
-            nc.sync.dma_start(out=raw_0[b][QUADRANT:WIDE_PARTS], in_=four_rows_a_partition(h_dn[b]))
-            nc.sync.dma_start(out=raw_0[b][0:QUADRANT], in_=four_rows_a_partition(xg2[b, 2 * P : WIDE_CH]))
-            nc.sync.dma_start(out=raw_0[b][WIDE_PARTS:P], in_=four_rows_a_partition(xg1[b, 0:P]))
+            rows = inputs.tile([P, PACK, NODES], BF16, name="pass_0_rows_%d" % b)
+            nc.sync.dma_start(out=rows[QUADRANT:WIDE_PARTS], in_=four_rows_a_partition(h_dn[b]))
+            nc.sync.dma_start(out=rows[0:QUADRANT], in_=four_rows_a_partition(xg2[b, 2 * P : WIDE_CH]))
+            nc.sync.dma_start(out=rows[WIDE_PARTS:P], in_=four_rows_a_partition(xg1[b, 0:P]))
+            pass_0_rows.append(rows)
 
         def load_h_rows(b):
-            h_rows[b] = inputs.tile([P, OUT_TILES, NODES], BF16, name="h_rows_%d" % b)
-            nc.sync.dma_start(out=h_rows[b][:], in_=h_dn[b].rearrange("(t o) n -> o t n", o=P))
+            rows = inputs.tile([P, OUT_TILES, NODES], BF16, name="h_rows_%d" % b)
+            nc.sync.dma_start(out=rows[:], in_=two_rows_a_partition(h_dn[b]))
+            h_rows.append(rows)
 
-        adj_raw = const.tile([P, NODE_CHUNKS, NODES], BF16)
-        w_raw = const.tile([P, GATE_TILES, Z_CH], BF16)
-        bias_rows = const.tile([P, P], BF16)
-        nc.vector.memset(bias_rows[:], 0.0)
+        adj_rows = const.tile([P, NODE_CHUNKS, NODES], BF16)
+        weight_rows = {}
+        bias = {}
 
-        def load_weights(weight, g):
-            rows = weight.rearrange("(t o) k -> o t k", o=P)
-            xg2_end = 3 * P + 2 * WIDE_CH
+        def load_adj():
+            nc.sync.dma_start(out=adj_rows[:], in_=adj.rearrange("(c w) v -> w c v", w=P))
+
+        def load_bias(gate, vector):
+            bias[gate] = const.tile([P, OUT_TILES], BF16, name="bias_%d" % gate)
+            nc.sync.dma_start(out=bias[gate][:], in_=vector.rearrange("(o t) -> o t", t=OUT_TILES))
+
+        def load_weights(gate, weight):
+            tile = const.tile([P, OUT_TILES, Z_CH], BF16, name="weight_rows_%d" % gate)
+            rows = weight.rearrange("(o t) k -> o t k", t=OUT_TILES)
+            xg3_start = Z_CH - WIDE_CH
             for to, first, end in (
                 (P, P, 2 * K_PASS),
-                (0, 2 * K_PASS, xg2_end),
-                (2 * K_PASS, xg2_end, Z_CH),
+                (0, 2 * K_PASS, xg3_start),
+                (2 * K_PASS, xg3_start, Z_CH),
                 (Z_CH - P, 0, P),
             ):
-                nc.sync.dma_start(
-                    out=w_raw[:, g : g + OUT_TILES, to : to + end - first], in_=rows[:, :, first:end]
-                )
+                nc.sync.dma_start(out=tile[:, :, to : to + end - first], in_=rows[:, :, first:end])
+            weight_rows[gate] = tile
 
-        def load_bias():
-            nc.sync.dma_start(out=bias_rows[0:OUT_TILES, :], in_=b_u.rearrange("(r o) -> r o", o=P))
-            nc.sync.dma_start(out=bias_rows[OUT_TILES:GATE_TILES, :], in_=b_c.rearrange("(r o) -> r o", o=P))
-
-        nc.sync.dma_start(out=x_raw[:], in_=four_rows_a_partition(x.rearrange("b c n -> (b c) n")))
-        load_pass_1(0)
-        nc.sync.dma_start(out=adj_raw[:], in_=adj.rearrange("(c w) v -> w c v", w=P))
-        load_pass_0(0)
-        load_bias()
-        load_weights(W_c, OUT_TILES)
-        load_pass_1(1)
-        load_weights(W_u, 0)
-
-        def turn(sources, word_order):
+        def transpose(sources, word_order):
             turned = psum.tile([P, 2, 2, P], F32, tag="bank")
             for a, source in enumerate(sources):
                 words = source.bitcast(F32).rearrange(word_order, u=2)
                 for u in range(2):
-                    nc.tensor.transpose(turned[:, a, u, :], words[:, u, :], ident_f32[:])
+                    nc.tensor.transpose(turned[:, a, u, :], words[:, u, :], identity[:])
             return turned
 
         def k_onto_partitions(sources, grouped, word_order):
-            turned = turn(sources, word_order)
+            turned = transpose(sources, word_order)
             nc.scalar.copy(out=grouped.bitcast(F32), in_=turned[:].rearrange("p a u r -> p a r u"))
 
         adj_grouped = const.tile([P, NODE_CHUNKS, P, PACK], BF16, align_bytes=64)
@@ -138,7 +139,7 @@ def tile_gcgrucell_epsilon_pb_kernel(tc, x, h_dn, xg1, xg2, adj, W_u, b_u, W_c, 
 
         def turn_adj():
             for c in range(0, NODE_CHUNKS, 2):
-                k_onto_partitions([adj_raw[:, c, :], adj_raw[:, c + 1, :]], adj_grouped[:, c : c + 2], HALVES)
+                k_onto_partitions([adj_rows[:, c, :], adj_rows[:, c + 1, :]], adj_grouped[:, c : c + 2], HALVES)
 
         def quantise_adj():
             nc.vector.quantize_mx(
@@ -147,204 +148,175 @@ def tile_gcgrucell_epsilon_pb_kernel(tc, x, h_dn, xg1, xg2, adj, W_u, b_u, W_c, 
                 in_=adj_grouped[:].rearrange("p c w t -> p (c w t)"),
             )
 
-        hop_grouped_tiles = []
+        hop_grouped = []
         for i in range(2):
-            tile = const.tile([P, PACK, P, PACK], BF16, name="hop_grouped_%d" % i, align_bytes=64)
-            nc.gpsimd.memset(tile[:, :, WIDE_PARTS:P], 0.0)
-            hop_grouped_tiles.append(tile)
+            grouped = const.tile([P, PACK, P, PACK], BF16, name="hop_grouped_%d" % i, align_bytes=64)
+            nc.gpsimd.memset(grouped[:, :, WIDE_PARTS:P], 0.0)
+            hop_grouped.append(grouped)
 
         def turn_xg2(b):
-            grouped = hop_grouped_tiles[b % 2]
-            words = grouped[:].rearrange("p j m t -> p (j m t)").bitcast(F32).rearrange("p (j m u) -> p j m u", j=PACK, u=2)
-            turned = turn([raw_1[b][:, 2, :], raw_1[b][:, 3, :]], HALVES)
+            words = hop_grouped[b % 2][:].rearrange("p j m t -> p (j m t)").bitcast(F32)
+            words = words.rearrange("p (j m u) -> p j m u", j=PACK, u=2)
+            turned = transpose([pass_1_rows[b][:, 2, :], pass_1_rows[b][:, 3, :]], HALVES)
             by_half = turned[:].rearrange("p e u (m h) -> p h e m u", h=2)
             for h in range(2):
                 nc.scalar.copy(out=words[:, 2 * h : 2 * h + 2, 0 : P // 2], in_=by_half[:, h])
-            turned = turn([xg2_rows[b][:]], HALVES)
+            turned = transpose([xg2_rows[b][:]], HALVES)
             nc.scalar.copy(
                 out=words[:, :, P // 2 : WIDE_PARTS], in_=turned[:, 0].rearrange("p u (q j) -> p j q u", j=PACK)
             )
-            return grouped
 
-        def quantise_turned_xg2(grouped):
-            codes = batches.tile([P, PACK, P], U32, name="hop_codes", align_bytes=64)
-            scales = batches.tile([P, PACK, P], U8, name="hop_scales", align_bytes=64)
+        hop_codes, hop_scales = {}, {}
+
+        def quantise_turned_xg2(b):
+            hop_codes[b] = batches.tile([P, PACK, P], U32, name="hop_codes", align_bytes=64)
+            hop_scales[b] = batches.tile([P, PACK, P], U8, name="hop_scales", align_bytes=64)
             nc.vector.quantize_mx(
-                out=codes[:].rearrange("p j m -> p (j m)").bitcast(FP8X4),
-                scales=scales[:].rearrange("p j m -> p (j m)"),
-                in_=grouped[:].rearrange("p j m t -> p (j m t)"),
+                out=hop_codes[b][:].rearrange("p j m -> p (j m)").bitcast(FP8X4),
+                scales=hop_scales[b][:].rearrange("p j m -> p (j m)"),
+                in_=hop_grouped[b % 2][:].rearrange("p j m t -> p (j m t)"),
             )
-            return codes, scales
 
         w_grouped = const.tile([P, 2, PASSES, OUT_TILES, P, PACK], BF16, align_bytes=64)
         w_codes = const.tile([P, 2, PASSES, OUT_TILES, P], U32, align_bytes=64)
         w_scales = const.tile([P, 2, PASSES, OUT_TILES, P], U8, align_bytes=64)
 
-        def turn_weights(g):
+        def turn_weights(gate):
             for s in range(PASSES):
+                columns = slice(s * K_PASS, (s + 1) * K_PASS)
                 k_onto_partitions(
-                    [w_raw[:, g + t, s * K_PASS : (s + 1) * K_PASS] for t in range(OUT_TILES)],
-                    w_grouped[:, g // 2, s],
+                    [weight_rows[gate][:, t, columns] for t in range(OUT_TILES)],
+                    w_grouped[:, gate, s],
                     HALVES if s == 1 else ALTERNATE,
                 )
 
-        def quantise_weights(g):
+        def quantise_weights(gate):
             for s in (slice(0, 2), slice(2, PASSES)):
                 nc.vector.quantize_mx(
-                    out=w_codes[:, g // 2, s].rearrange("p s g o -> p (s g o)").bitcast(FP8X4),
-                    scales=w_scales[:, g // 2, s].rearrange("p s g o -> p (s g o)"),
-                    in_=w_grouped[:, g // 2, s].rearrange("p s g o t -> p (s g o t)"),
+                    out=w_codes[:, gate, s].rearrange("p s t o -> p (s t o)").bitcast(FP8X4),
+                    scales=w_scales[:, gate, s].rearrange("p s t o -> p (s t o)"),
+                    in_=w_grouped[:, gate, s].rearrange("p s t o k -> p (s t o k)"),
                 )
 
-        bias = const.tile([P, GATE_TILES], F32)
-
-        def spread_bias():
-            bias_turned = psum.tile([P, P], BF16, tag="bank")
-            nc.tensor.transpose(bias_turned[:], bias_rows[:], ident_bf16[:])
-            nc.vector.tensor_copy(out=bias[:], in_=bias_turned[:, 0:GATE_TILES])
-
-        def side_by_side(copy, grouped, raw):
+        def side_by_side(copy, words, rows):
             copy(
-                out=grouped.rearrange("p (c i) j -> p c j i", i=4),
-                in_=raw.rearrange("p j (c i) -> p c j i", i=4),
+                out=words.rearrange("p (c i) j -> p c j i", i=4),
+                in_=rows.rearrange("p j (c i) -> p c j i", i=4),
             )
 
-        def quantise_loaded_passes(grouped):
-            codes = batches.tile([P, 2, NODES], U32, name="z01_codes", align_bytes=64)
-            scales = batches.tile([P, 2, NODES], U8, name="z01_scales", align_bytes=64)
+        def regroup_x():
+            side_by_side(nc.vector.tensor_copy, x_words[:], x_rows[:])
+
+        def regroup_pass_1(b):
+            side_by_side(nc.vector.tensor_copy, pass_01_words[b][:, 1], pass_1_rows[b][:])
+
+        def regroup_pass_0(b, copy, nodes=slice(0, NODES)):
+            side_by_side(copy, pass_01_words[b][:, 0, nodes], pass_0_rows[b][:, :, nodes])
+
+        pass_01, pass_2 = {}, {}
+
+        def quantise_pass_01(b):
+            codes = batches.tile([P, 2, NODES], U32, name="pass_01_codes", align_bytes=64)
+            scales = batches.tile([P, 2, NODES], U8, name="pass_01_scales", align_bytes=64)
             nc.vector.quantize_mx(
                 out=codes[:].rearrange("p s n -> p (s n)").bitcast(FP8X4),
                 scales=scales[:].rearrange("p s n -> p (s n)"),
-                in_=grouped[:].rearrange("p s n t -> p (s n t)"),
+                in_=pass_01_words[b][:].rearrange("p s n t -> p (s n t)"),
             )
-            return codes, scales
+            pass_01[b] = codes, scales
 
-        def hop_products(hop_codes, hop_scales):
+        def hop(b):
             banks = []
             for c in range(NODE_CHUNKS):
-                cols = slice(c * P, (c + 1) * P)
+                nodes = slice(c * P, (c + 1) * P)
                 hopped = psum.tile([P, PACK, P], F32, name="hopped_%d" % c, tag="bank")
                 for j in range(PACK):
                     nc.tensor.matmul_mx(
                         out=hopped[:, j, :],
-                        lhsT=hop_codes[:, j, :].bitcast(FP8X4),
-                        lhsT_scale=hop_scales[:, j, :],
-                        rhs=adj_codes[:, cols].bitcast(FP8X4),
-                        rhs_scale=adj_scales[:, cols],
+                        lhsT=hop_codes[b][:, j, :].bitcast(FP8X4),
+                        lhsT_scale=hop_scales[b][:, j, :],
+                        rhs=adj_codes[:, nodes].bitcast(FP8X4),
+                        rhs_scale=adj_scales[:, nodes],
                         start=True,
                         stop=True,
                     )
                 banks.append(hopped)
-            return banks
-
-        def round_hop(banks, z2_grouped):
             for c in range(NODE_CHUNKS):
                 nc.scalar.copy(
-                    out=z2_grouped[0:WIDE_PARTS, c * P : (c + 1) * P, :],
+                    out=pass_2_words[b][0:WIDE_PARTS, c * P : (c + 1) * P, :],
                     in_=banks[c][0:WIDE_PARTS].rearrange("p j w -> p w j"),
                 )
 
-        def quantise_hop_pass(z2_grouped):
-            codes = batches.tile([P, NODES], U32, name="z2_codes", align_bytes=64)
-            scales = batches.tile([P, NODES], U8, name="z2_scales", align_bytes=64)
+        def quantise_pass_2(b):
+            codes = batches.tile([P, NODES], U32, name="pass_2_codes", align_bytes=64)
+            scales = batches.tile([P, NODES], U8, name="pass_2_scales", align_bytes=64)
             nc.vector.quantize_mx(
                 out=codes[:].bitcast(FP8X4),
                 scales=scales[:],
-                in_=z2_grouped[:].rearrange("p n t -> p (n t)"),
+                in_=pass_2_words[b][:].rearrange("p n t -> p (n t)"),
             )
-            return codes, scales
+            pass_2[b] = codes, scales
 
-        def gate_sums(z_operands):
-            sums = {}
-            for g in GATE_ORDER:
-                sums[g] = psum.tile([P, NODES], F32, name="sums_%d" % g, tag="bank")
-                for s in range(PASSES):
-                    z_codes, z_scales = z_operands[s]
+        gated = {}
+
+        def gates(b):
+            codes, scales = pass_01[b]
+            z_operands = [(codes[:, s, :], scales[:, s, :]) for s in range(2)]
+            z_operands.append((pass_2[b][0][:], pass_2[b][1][:]))
+            sums = []
+            for gate, t in GATE_ORDER:
+                bank = psum.tile([P, NODES], F32, name="sums_%d_%d" % (gate, t), tag="bank")
+                for s, (z_codes, z_scales) in enumerate(z_operands):
                     nc.tensor.matmul_mx(
-                        out=sums[g][:],
-                        lhsT=w_codes[:, g // OUT_TILES, s, g % OUT_TILES, :].bitcast(FP8X4),
-                        lhsT_scale=w_scales[:, g // OUT_TILES, s, g % OUT_TILES, :],
+                        out=bank[:],
+                        lhsT=w_codes[:, gate, s, t, :].bitcast(FP8X4),
+                        lhsT_scale=w_scales[:, gate, s, t, :],
                         rhs=z_codes.bitcast(FP8X4),
                         rhs_scale=z_scales,
                         start=(s == 0),
                         stop=(s == PASSES - 1),
                     )
-            return sums
-
-        def gate_functions(sums, between):
-            gate = batches.tile([P, GATE_TILES, NODES], F32, name="gate")
-            for i, g in enumerate(GATE_ORDER):
+                sums.append(bank)
+            gated[b] = batches.tile([P, 2, OUT_TILES, NODES], F32, name="gated")
+            for (gate, t), bank in zip(GATE_ORDER, sums):
                 nc.scalar.activation(
-                    out=gate[:, g, :],
-                    in_=sums[g][:],
-                    func=(ACT.Sigmoid if g < OUT_TILES else ACT.Tanh),
-                    bias=bias[:, g : g + 1],
+                    out=gated[b][:, gate, t, :],
+                    in_=bank[:],
+                    func=(ACT.Sigmoid if gate == UPDATE else ACT.Tanh),
+                    bias=bias[gate][:, t : t + 1],
                     scale=1.0,
                 )
-                between(i)
-            return gate
 
-        mixed = {}
-
-        def blend_difference(b, t):
-            if b not in mixed:
-                mixed[b] = batches.tile([P, OUT_TILES, NODES], F32, name="mixed")
-            candidate = gate[b][:, OUT_TILES:GATE_TILES]
-            nc.vector.tensor_tensor(out=mixed[b][:, t], in0=h_rows[b][:, t], in1=candidate[:, t], op=ALU.subtract)
-
-        def blend_product(b, t):
-            update = gate[b][:, 0:OUT_TILES]
-            nc.vector.tensor_tensor(out=mixed[b][:, t], in0=mixed[b][:, t], in1=update[:, t], op=ALU.mult)
-
-        def blend_sum(b, t, nodes=slice(0, NODES)):
-            candidate = gate[b][:, OUT_TILES:GATE_TILES, nodes]
-            result = mixed[b][:, t, nodes]
-            nc.vector.tensor_tensor(out=result, in0=result, in1=candidate[:, t], op=ALU.add)
-            rows = out[b].rearrange("(t o) n -> o t n", o=P)
-            nc.sync.dma_start(out=rows[:, t, nodes], in_=result)
-
-        hop_grouped, hop_operands, hop_banks, z01_grouped, z01, z2 = {}, {}, {}, {}, {}, {}
-
-        def turn_hop(b):
-            hop_grouped[b] = turn_xg2(b)
-
-        def hop(b):
-            round_hop(hop_products(*hop_operands[b]), z2_grouped[b])
-
-        for b in range(BATCH):
-            z01_grouped[b] = batches.tile([P, 2, NODES, PACK], BF16, name="z01_grouped", align_bytes=64)
-
-        def regroup_xg2(b):
-            side_by_side(nc.vector.tensor_copy, z01_grouped[b][:, 1], raw_1[b][:])
-
-        def regroup_xg1(b, copy, nodes=slice(0, NODES)):
-            side_by_side(copy, z01_grouped[b][:, 0, nodes], raw_0[b][:, :, nodes])
-
-        def quantise_hop_operand(b):
-            hop_operands[b] = quantise_turned_xg2(hop_grouped[b])
-
-        def quantise_z01(b):
-            z01[b] = quantise_loaded_passes(z01_grouped[b])
-
-        def quantise_z2(b):
-            z2[b] = quantise_hop_pass(z2_grouped[b])
-
-        gate = {}
-
-        def gates(b, between=lambda i: None):
-            sums = gate_sums(
-                [
-                    (z01[b][0][:, 0, :], z01[b][1][:, 0, :]),
-                    (z01[b][0][:, 1, :], z01[b][1][:, 1, :]),
-                    (z2[b][0][:], z2[b][1][:]),
-                ]
-            )
-            gate[b] = gate_functions(sums, between)
-
+        mixed = [batches.tile([P, OUT_TILES, NODES], F32, name="mixed") for b in range(BATCH)]
         both = slice(0, OUT_TILES)
+
+        def blend_difference(b, t=both):
+            nc.vector.tensor_tensor(
+                out=mixed[b][:, t], in0=h_rows[b][:, t], in1=gated[b][:, CANDIDATE, t], op=ALU.subtract
+            )
+
+        def blend_product(b, t=both):
+            nc.vector.tensor_tensor(out=mixed[b][:, t], in0=mixed[b][:, t], in1=gated[b][:, UPDATE, t], op=ALU.mult)
+
+        def blend_sum(b, t=both, nodes=slice(0, NODES)):
+            result = mixed[b][:, t, nodes]
+            nc.vector.tensor_tensor(out=result, in0=result, in1=gated[b][:, CANDIDATE, t, nodes], op=ALU.add)
+            nc.sync.dma_start(out=two_rows_a_partition(out[b])[:, t, nodes], in_=result)
+
         low, high = slice(0, NODES // 2), slice(NODES // 2, NODES)
+
+        load_x()
+        load_pass_1(0)
+        load_adj()
+        load_pass_0(0)
+        load_bias(UPDATE, b_u)
+        load_bias(CANDIDATE, b_c)
+        load_weights(CANDIDATE, W_c)
+        load_pass_1(1)
+        load_weights(UPDATE, W_u)
+
         keep_tensor_busy(6)
-        side_by_side(nc.vector.tensor_copy, x_grouped[:], x_raw[:])
+        regroup_x()
         move_x(0)
         load_pass_0(1)
         load_pass_1(2)
@@ -354,64 +326,65 @@ def tile_gcgrucell_epsilon_pb_kernel(tc, x, h_dn, xg1, xg2, adj, W_u, b_u, W_c, 
         load_pass_1(3)
         move_x(2)
         load_pass_0(3)
-        load_h_rows(1)
-        load_h_rows(2)
-        load_h_rows(3)
-        turn_hop(0)
+        for b in range(1, BATCH):
+            load_h_rows(b)
+        turn_xg2(0)
         keep_tensor_busy(2)
-        regroup_xg2(0)
-        quantise_hop_operand(0)
-        regroup_xg1(0, nc.vector.tensor_copy, low)
+        regroup_pass_1(0)
+        quantise_turned_xg2(0)
+        regroup_pass_0(0, nc.vector.tensor_copy, low)
         turn_adj()
-        keep_tensor_busy(2)
-        regroup_xg1(0, nc.scalar.copy, high)
+        keep_tensor_busy(4)
+        regroup_pass_0(0, nc.scalar.copy, high)
         quantise_adj()
         hop(0)
-        quantise_z01(0)
-        regroup_xg2(1)
-        turn_hop(1)
+        quantise_pass_01(0)
+        regroup_pass_1(1)
+        turn_xg2(1)
         keep_tensor_busy(2)
-        turn_weights(OUT_TILES)
+        turn_weights(CANDIDATE)
         keep_tensor_busy(2)
-        quantise_hop_operand(1)
-        quantise_weights(OUT_TILES)
-        quantise_z2(0)
-        turn_weights(0)
-        quantise_weights(0)
-        spread_bias()
+        quantise_turned_xg2(1)
+        quantise_weights(CANDIDATE)
+        quantise_pass_2(0)
+        turn_weights(UPDATE)
+        quantise_weights(UPDATE)
+
         hop(1)
-        regroup_xg1(1, nc.vector.tensor_copy)
+        regroup_pass_0(1, nc.vector.tensor_copy)
         gates(0)
-        quantise_z01(1)
-        turn_hop(2)
-        regroup_xg2(2)
-        quantise_z2(1)
+        quantise_pass_01(1)
+        turn_xg2(2)
+        regroup_pass_1(2)
+        quantise_pass_2(1)
         gates(1)
-        blend_difference(0, both)
-        quantise_hop_operand(2)
-        blend_product(0, both)
-        turn_hop(3)
+        blend_difference(0)
+        quantise_turned_xg2(2)
+        blend_product(0)
+
+        turn_xg2(3)
         hop(2)
-        regroup_xg1(2, nc.vector.tensor_copy)
-        blend_sum(0, both)
-        quantise_z01(2)
-        regroup_xg2(3)
-        quantise_hop_operand(3)
-        quantise_z2(2)
-        regroup_xg1(3, nc.scalar.copy, high)
+        regroup_pass_0(2, nc.vector.tensor_copy)
+        blend_sum(0)
+        quantise_pass_01(2)
+        regroup_pass_1(3)
+        quantise_turned_xg2(3)
+        quantise_pass_2(2)
+        regroup_pass_0(3, nc.scalar.copy, slice(P, NODES))
         hop(3)
         gates(2)
-        blend_difference(1, both)
-        regroup_xg1(3, nc.vector.tensor_copy, low)
-        blend_product(1, both)
-        quantise_z01(3)
-        quantise_z2(3)
+        blend_difference(1)
+        regroup_pass_0(3, nc.vector.tensor_copy, slice(0, P))
+        blend_product(1)
+        quantise_pass_01(3)
+        quantise_pass_2(3)
+
         gates(3)
-        blend_sum(1, both)
-        blend_difference(2, both)
-        blend_product(2, both)
+        blend_sum(1)
+        blend_difference(2)
+        blend_product(2)
         blend_difference(3, 0)
-        blend_sum(2, both)
+        blend_sum(2)
         blend_difference(3, 1)
         blend_product(3, 0)
         blend_product(3, 1)

from contextlib import ExitStack

import concourse.mybir as mybir
from concourse.masks import make_identity

F32 = mybir.dt.float32
BF16 = mybir.dt.bfloat16
U32 = mybir.dt.uint32
U8 = mybir.dt.uint8
FP8X4 = mybir.dt.float8_e4m3fn_x4
ACT = mybir.ActivationFunctionType
ALU = mybir.AluOpType

P = 128
PACK = 4
K_PASS = P * PACK
BATCH = 4
NODES = 512
NODE_CHUNKS = NODES // P
WIDE_CH = 384
WIDE_PARTS = WIDE_CH // PACK
QUADRANT = 32
OUT_TILES = 2
UPDATE, CANDIDATE = 0, 1
PASSES = 3
Z_CH = PASSES * K_PASS
PSUM_BANKS = 8
ALTERNATE = "r (p u) -> r u p"
HALVES = "r (u p) -> r u p"
GATE_ORDER = ((CANDIDATE, 0), (CANDIDATE, 1), (UPDATE, 0), (UPDATE, 1))

FLOPS = 2 * BATCH * WIDE_CH * NODES * NODES + 2 * 2 * BATCH * OUT_TILES * P * Z_CH * NODES


def tile_gcgrucell_epsilon_pb_kernel(tc, x, h_dn, xg1, xg2, adj, W_u, b_u, W_c, b_c, out):
    nc = tc.nc
    with ExitStack() as ctx:
        ctx.enter_context(tc.manual_schedule())
        const = ctx.enter_context(tc.tile_pool(name="const", bufs=1))
        inputs = ctx.enter_context(tc.tile_pool(name="inputs", bufs=1))
        batches = ctx.enter_context(tc.tile_pool(name="batches", bufs=BATCH))
        psum = ctx.enter_context(tc.psum_pool(name="psum", bufs=PSUM_BANKS))

        identity = const.tile([P, P], F32)
        make_identity(nc, identity[:])

        warm = const.tile([P, 1], F32)
        nc.vector.memset(warm[:], 0.0)
        nc.scalar.activation(out=warm[:], in_=warm[:], func=ACT.Sigmoid)

        zeros = const.tile([P, NODES], BF16)
        nc.vector.memset(zeros[:], 0.0)

        def keep_tensor_busy(passes):
            idle = psum.tile([P, NODES], F32, name="idle", tag="bank")
            for i in range(passes):
                nc.tensor.matmul(idle[:], lhsT=zeros[:, 0:P], rhs=zeros[:], start=True, stop=True)

        def four_rows_a_partition(rows):
            return rows.rearrange("(p j) n -> p j n", j=PACK)

        def two_rows_a_partition(rows):
            return rows.rearrange("(p e) n -> p e n", e=2)

        pass_0_rows, pass_1_rows, xg2_rows, h_rows = [], [], [], []
        x_rows = const.tile([P, PACK, NODES], BF16)
        pass_01_words = [
            batches.tile([P, 2, NODES, PACK], BF16, name="pass_01_words", align_bytes=64) for b in range(BATCH)
        ]
        pass_2_words = [batches.tile([P, NODES, PACK], BF16, name="pass_2_words", align_bytes=64) for b in range(BATCH)]
        x_words = pass_2_words[BATCH - 1]

        def load_x():
            nc.sync.dma_start(out=x_rows[:], in_=four_rows_a_partition(x.rearrange("b c n -> (b c) n")))

        def move_x(b):
            nc.sync.dma_start(out=pass_2_words[b][WIDE_PARTS:P], in_=x_words[b * QUADRANT : (b + 1) * QUADRANT])

        def load_pass_1(b):
            rows = inputs.tile([P, PACK, NODES], BF16, name="pass_1_rows_%d" % b)
            nc.sync.dma_start(out=rows[:, 2:PACK], in_=two_rows_a_partition(xg2[b, 0 : 2 * P]))
            last_third = inputs.tile([P, NODES], BF16, name="xg2_rows_%d" % b)
            nc.sync.dma_start(out=last_third[:], in_=xg2[b, 2 * P : WIDE_CH])
            nc.sync.dma_start(out=rows[:, 0:2], in_=two_rows_a_partition(xg1[b, P:WIDE_CH]))
            pass_1_rows.append(rows)
            xg2_rows.append(last_third)

        def load_pass_0(b):
            rows = inputs.tile([P, PACK, NODES], BF16, name="pass_0_rows_%d" % b)
            nc.sync.dma_start(out=rows[QUADRANT:WIDE_PARTS], in_=four_rows_a_partition(h_dn[b]))
            nc.sync.dma_start(out=rows[0:QUADRANT], in_=four_rows_a_partition(xg2[b, 2 * P : WIDE_CH]))
            nc.sync.dma_start(out=rows[WIDE_PARTS:P], in_=four_rows_a_partition(xg1[b, 0:P]))
            pass_0_rows.append(rows)

        def load_h_rows(b):
            rows = inputs.tile([P, OUT_TILES, NODES], BF16, name="h_rows_%d" % b)
            nc.sync.dma_start(out=rows[:], in_=two_rows_a_partition(h_dn[b]))
            h_rows.append(rows)

        adj_rows = const.tile([P, NODE_CHUNKS, NODES], BF16)
        weight_rows = {}
        bias = {}

        def load_adj():
            nc.sync.dma_start(out=adj_rows[:], in_=adj.rearrange("(c w) v -> w c v", w=P))

        def load_bias(gate, vector):
            bias[gate] = const.tile([P, OUT_TILES], BF16, name="bias_%d" % gate)
            nc.sync.dma_start(out=bias[gate][:], in_=vector.rearrange("(o t) -> o t", t=OUT_TILES))

        def load_weights(gate, weight):
            tile = const.tile([P, OUT_TILES, Z_CH], BF16, name="weight_rows_%d" % gate)
            rows = weight.rearrange("(o t) k -> o t k", t=OUT_TILES)
            xg3_start = Z_CH - WIDE_CH
            for to, first, end in (
                (P, P, 2 * K_PASS),
                (0, 2 * K_PASS, xg3_start),
                (2 * K_PASS, xg3_start, Z_CH),
                (Z_CH - P, 0, P),
            ):
                nc.sync.dma_start(out=tile[:, :, to : to + end - first], in_=rows[:, :, first:end])
            weight_rows[gate] = tile

        def transpose(sources, word_order):
            turned = psum.tile([P, 2, 2, P], F32, tag="bank")
            for a, source in enumerate(sources):
                words = source.bitcast(F32).rearrange(word_order, u=2)
                for u in range(2):
                    nc.tensor.transpose(turned[:, a, u, :], words[:, u, :], identity[:])
            return turned

        def k_onto_partitions(sources, grouped, word_order):
            turned = transpose(sources, word_order)
            nc.scalar.copy(out=grouped.bitcast(F32), in_=turned[:].rearrange("p a u r -> p a r u"))

        adj_grouped = const.tile([P, NODE_CHUNKS, P, PACK], BF16, align_bytes=64)
        adj_codes = const.tile([P, NODES], U32, align_bytes=64)
        adj_scales = const.tile([P, NODES], U8, align_bytes=64)

        def turn_adj():
            for c in range(0, NODE_CHUNKS, 2):
                k_onto_partitions([adj_rows[:, c, :], adj_rows[:, c + 1, :]], adj_grouped[:, c : c + 2], HALVES)

        def quantise_adj():
            nc.vector.quantize_mx(
                out=adj_codes[:].bitcast(FP8X4),
                scales=adj_scales[:],
                in_=adj_grouped[:].rearrange("p c w t -> p (c w t)"),
            )

        hop_grouped = []
        for i in range(2):
            grouped = const.tile([P, PACK, P, PACK], BF16, name="hop_grouped_%d" % i, align_bytes=64)
            nc.gpsimd.memset(grouped[:, :, WIDE_PARTS:P], 0.0)
            hop_grouped.append(grouped)

        def turn_xg2(b):
            words = hop_grouped[b % 2][:].rearrange("p j m t -> p (j m t)").bitcast(F32)
            words = words.rearrange("p (j m u) -> p j m u", j=PACK, u=2)
            turned = transpose([pass_1_rows[b][:, 2, :], pass_1_rows[b][:, 3, :]], HALVES)
            by_half = turned[:].rearrange("p e u (m h) -> p h e m u", h=2)
            for h in range(2):
                nc.scalar.copy(out=words[:, 2 * h : 2 * h + 2, 0 : P // 2], in_=by_half[:, h])
            turned = transpose([xg2_rows[b][:]], HALVES)
            nc.scalar.copy(
                out=words[:, :, P // 2 : WIDE_PARTS], in_=turned[:, 0].rearrange("p u (q j) -> p j q u", j=PACK)
            )

        hop_codes, hop_scales = {}, {}

        def quantise_turned_xg2(b):
            hop_codes[b] = batches.tile([P, PACK, P], U32, name="hop_codes", align_bytes=64)
            hop_scales[b] = batches.tile([P, PACK, P], U8, name="hop_scales", align_bytes=64)
            nc.vector.quantize_mx(
                out=hop_codes[b][:].rearrange("p j m -> p (j m)").bitcast(FP8X4),
                scales=hop_scales[b][:].rearrange("p j m -> p (j m)"),
                in_=hop_grouped[b % 2][:].rearrange("p j m t -> p (j m t)"),
            )

        w_grouped = const.tile([P, 2, PASSES, OUT_TILES, P, PACK], BF16, align_bytes=64)
        w_codes = const.tile([P, 2, PASSES, OUT_TILES, P], U32, align_bytes=64)
        w_scales = const.tile([P, 2, PASSES, OUT_TILES, P], U8, align_bytes=64)

        def turn_weights(gate):
            for s in range(PASSES):
                columns = slice(s * K_PASS, (s + 1) * K_PASS)
                k_onto_partitions(
                    [weight_rows[gate][:, t, columns] for t in range(OUT_TILES)],
                    w_grouped[:, gate, s],
                    HALVES if s == 1 else ALTERNATE,
                )

        def quantise_weights(gate):
            for s in (slice(0, 2), slice(2, PASSES)):
                nc.vector.quantize_mx(
                    out=w_codes[:, gate, s].rearrange("p s t o -> p (s t o)").bitcast(FP8X4),
                    scales=w_scales[:, gate, s].rearrange("p s t o -> p (s t o)"),
                    in_=w_grouped[:, gate, s].rearrange("p s t o k -> p (s t o k)"),
                )

        def side_by_side(copy, words, rows):
            copy(
                out=words.rearrange("p (c i) j -> p c j i", i=4),
                in_=rows.rearrange("p j (c i) -> p c j i", i=4),
            )

        def regroup_x():
            side_by_side(nc.vector.tensor_copy, x_words[:], x_rows[:])

        def regroup_pass_1(b):
            side_by_side(nc.vector.tensor_copy, pass_01_words[b][:, 1], pass_1_rows[b][:])

        def regroup_pass_0(b, copy, nodes=slice(0, NODES)):
            side_by_side(copy, pass_01_words[b][:, 0, nodes], pass_0_rows[b][:, :, nodes])

        pass_01, pass_2 = {}, {}

        def quantise_pass_01(b):
            codes = batches.tile([P, 2, NODES], U32, name="pass_01_codes", align_bytes=64)
            scales = batches.tile([P, 2, NODES], U8, name="pass_01_scales", align_bytes=64)
            nc.vector.quantize_mx(
                out=codes[:].rearrange("p s n -> p (s n)").bitcast(FP8X4),
                scales=scales[:].rearrange("p s n -> p (s n)"),
                in_=pass_01_words[b][:].rearrange("p s n t -> p (s n t)"),
            )
            pass_01[b] = codes, scales

        def hop(b):
            banks = []
            for c in range(NODE_CHUNKS):
                nodes = slice(c * P, (c + 1) * P)
                hopped = psum.tile([P, PACK, P], F32, name="hopped_%d" % c, tag="bank")
                for j in range(PACK):
                    nc.tensor.matmul_mx(
                        out=hopped[:, j, :],
                        lhsT=hop_codes[b][:, j, :].bitcast(FP8X4),
                        lhsT_scale=hop_scales[b][:, j, :],
                        rhs=adj_codes[:, nodes].bitcast(FP8X4),
                        rhs_scale=adj_scales[:, nodes],
                        start=True,
                        stop=True,
                    )
                banks.append(hopped)
            for c in range(NODE_CHUNKS):
                nc.scalar.copy(
                    out=pass_2_words[b][0:WIDE_PARTS, c * P : (c + 1) * P, :],
                    in_=banks[c][0:WIDE_PARTS].rearrange("p j w -> p w j"),
                )

        def quantise_pass_2(b):
            codes = batches.tile([P, NODES], U32, name="pass_2_codes", align_bytes=64)
            scales = batches.tile([P, NODES], U8, name="pass_2_scales", align_bytes=64)
            nc.vector.quantize_mx(
                out=codes[:].bitcast(FP8X4),
                scales=scales[:],
                in_=pass_2_words[b][:].rearrange("p n t -> p (n t)"),
            )
            pass_2[b] = codes, scales

        gated = {}

        def gates(b):
            codes, scales = pass_01[b]
            z_operands = [(codes[:, s, :], scales[:, s, :]) for s in range(2)]
            z_operands.append((pass_2[b][0][:], pass_2[b][1][:]))
            sums = []
            for gate, t in GATE_ORDER:
                bank = psum.tile([P, NODES], F32, name="sums_%d_%d" % (gate, t), tag="bank")
                for s, (z_codes, z_scales) in enumerate(z_operands):
                    nc.tensor.matmul_mx(
                        out=bank[:],
                        lhsT=w_codes[:, gate, s, t, :].bitcast(FP8X4),
                        lhsT_scale=w_scales[:, gate, s, t, :],
                        rhs=z_codes.bitcast(FP8X4),
                        rhs_scale=z_scales,
                        start=(s == 0),
                        stop=(s == PASSES - 1),
                    )
                sums.append(bank)
            gated[b] = batches.tile([P, 2, OUT_TILES, NODES], F32, name="gated")
            for (gate, t), bank in zip(GATE_ORDER, sums):
                nc.scalar.activation(
                    out=gated[b][:, gate, t, :],
                    in_=bank[:],
                    func=(ACT.Sigmoid if gate == UPDATE else ACT.Tanh),
                    bias=bias[gate][:, t : t + 1],
                    scale=1.0,
                )

        mixed = [batches.tile([P, OUT_TILES, NODES], F32, name="mixed") for b in range(BATCH)]
        both = slice(0, OUT_TILES)

        def blend_difference(b, t=both):
            nc.vector.tensor_tensor(
                out=mixed[b][:, t], in0=h_rows[b][:, t], in1=gated[b][:, CANDIDATE, t], op=ALU.subtract
            )

        def blend_product(b, t=both):
            nc.vector.tensor_tensor(out=mixed[b][:, t], in0=mixed[b][:, t], in1=gated[b][:, UPDATE, t], op=ALU.mult)

        def blend_sum(b, t=both, nodes=slice(0, NODES)):
            result = mixed[b][:, t, nodes]
            nc.vector.tensor_tensor(out=result, in0=result, in1=gated[b][:, CANDIDATE, t, nodes], op=ALU.add)
            nc.sync.dma_start(out=two_rows_a_partition(out[b])[:, t, nodes], in_=result)

        low, high = slice(0, NODES // 2), slice(NODES // 2, NODES)

        load_x()
        load_pass_1(0)
        load_adj()
        load_pass_0(0)
        load_bias(UPDATE, b_u)
        load_bias(CANDIDATE, b_c)
        load_weights(CANDIDATE, W_c)
        load_pass_1(1)
        load_weights(UPDATE, W_u)

        keep_tensor_busy(6)
        regroup_x()
        move_x(0)
        load_pass_0(1)
        load_pass_1(2)
        move_x(1)
        load_h_rows(0)
        load_pass_0(2)
        load_pass_1(3)
        move_x(2)
        load_pass_0(3)
        for b in range(1, BATCH):
            load_h_rows(b)
        turn_xg2(0)
        keep_tensor_busy(2)
        regroup_pass_1(0)
        quantise_turned_xg2(0)
        regroup_pass_0(0, nc.vector.tensor_copy, low)
        turn_adj()
        keep_tensor_busy(4)
        regroup_pass_0(0, nc.scalar.copy, high)
        quantise_adj()
        hop(0)
        quantise_pass_01(0)
        regroup_pass_1(1)
        turn_xg2(1)
        keep_tensor_busy(2)
        turn_weights(CANDIDATE)
        keep_tensor_busy(2)
        quantise_turned_xg2(1)
        quantise_weights(CANDIDATE)
        quantise_pass_2(0)
        turn_weights(UPDATE)
        quantise_weights(UPDATE)

        hop(1)
        regroup_pass_0(1, nc.vector.tensor_copy)
        gates(0)
        quantise_pass_01(1)
        turn_xg2(2)
        regroup_pass_1(2)
        quantise_pass_2(1)
        gates(1)
        blend_difference(0)
        quantise_turned_xg2(2)
        blend_product(0)

        turn_xg2(3)
        hop(2)
        regroup_pass_0(2, nc.vector.tensor_copy)
        blend_sum(0)
        quantise_pass_01(2)
        regroup_pass_1(3)
        quantise_turned_xg2(3)
        quantise_pass_2(2)
        regroup_pass_0(3, nc.scalar.copy, slice(P, NODES))
        hop(3)
        gates(2)
        blend_difference(1)
        regroup_pass_0(3, nc.vector.tensor_copy, slice(0, P))
        blend_product(1)
        quantise_pass_01(3)
        quantise_pass_2(3)

        gates(3)
        blend_sum(1)
        blend_difference(2)
        blend_product(2)
        blend_difference(3, 0)
        blend_sum(2)
        blend_difference(3, 1)
        blend_product(3, 0)
        blend_product(3, 1)
        blend_sum(3, 0)
        blend_sum(3, 1, low)
        blend_sum(3, 1, high)
